import numpy as np
import ml_dtypes


def mxq(x, axis, fmt="e4m3"):
    dtype, down = {"e4m3": (ml_dtypes.float8_e4m3fn, 7), "e5m2": (ml_dtypes.float8_e5m2, 14)}[fmt]
    v = np.moveaxis(np.asarray(x, np.float32).astype(ml_dtypes.bfloat16).astype(np.float64), axis, -1)
    blocks = v.reshape(v.shape[:-1] + (-1, 32))
    amax = np.abs(blocks).max(-1, keepdims=True)
    byte = np.maximum(np.where(amax > 0, np.frexp(amax)[1] - 1 + 127, 0) - down, 1)
    scale = np.exp2(byte - 127.0)
    codes = (blocks / scale).astype(np.float32).astype(dtype).astype(np.float64)
    return np.moveaxis((codes * scale).reshape(v.shape), -1, axis)


WIDE = False


def mx_kscale(k):
    if not WIDE:
        return np.ones(k)
    levels = np.array([10, -10, 5, -5, 0])
    if k % 512:
        return np.exp2(np.random.permutation(np.resize(levels, k // 32))).repeat(32)
    a = np.empty((k // 512, 16))
    for p in range(k // 512):
        a[p, :8] = np.random.permutation(np.resize(levels, 8))
        for g in range(8):
            far = levels[np.abs(levels - a[p, g]) >= 10]
            a[p, g + 8] = far[np.random.randint(len(far))]
    return np.exp2(a.ravel()).repeat(32)


BF16 = ml_dtypes.bfloat16


def bf(x):
    return np.asarray(x, np.float32).astype(BF16)


def f64(x):
    return np.asarray(x).astype(np.float64)


B, H, W, C, NH, WS, SHIFT, MR = 1, 64, 64, 256, 8, 32, 16, 4
HD = C // NH
WS2 = WS * WS
NWH, NWW = H // WS, W // WS
EPS = 1e-5
G2 = 0.1


def layer_norm(v, w, b):
    mu = v.mean(-1, keepdims=True)
    var = ((v - mu) ** 2).mean(-1, keepdims=True)
    return (v - mu) * (1.0 / np.sqrt(var + EPS)) * w + b


def setup_inputs():
    s = mx_kscale(WS2)
    u = (s / s.max()) ** 2
    um = np.tile(u.reshape(WS, WS), (NWH, NWW)).reshape(1, H * W, 1)
    d = u * np.sqrt((G2 + EPS) / (G2 * u * u + EPS))
    g = np.exp2(-7.5 * np.random.random_sample((B, H * W, 1)))
    x = (np.random.standard_normal((B, H * W, C)) + 0.5 * np.random.standard_normal((B, H * W, 1))) * g * um
    return {"x": bf(x),
            "norm1_w": bf(1.0 + 0.2 * np.random.standard_normal(C)),
            "norm1_b": bf(0.2 * np.random.standard_normal(C) * d.min()),
            "spatial_w": bf(np.random.standard_normal((NH, WS2, WS2)) / np.sqrt(WS2) / d[None, None, :]),
            "spatial_b": bf(0.3 * np.random.standard_normal((NH, WS2)))}


def reference(x, norm1_w, norm1_b, spatial_w, spatial_b):
    x = f64(x)
    xn = layer_norm(x, f64(norm1_w), f64(norm1_b))
    win = xn.reshape(B, NWH, WS, NWW, WS, C).transpose(0, 1, 3, 2, 4, 5).reshape(-1, WS2, NH, HD)
    wh = win.transpose(0, 2, 1, 3)
    out = (mxq(f64(spatial_w), 2, "e4m3")[None] @ mxq(wh, 2, "e4m3")) + f64(spatial_b)[None, :, :, None]
    w2 = out.transpose(0, 2, 1, 3).reshape(B, NWH, NWW, WS, WS, C)
    xs2 = w2.transpose(0, 1, 3, 2, 4, 5).reshape(B, H * W, C)
    return x + xs2

@@ -1,0 +1,289 @@
+from contextlib import ExitStack
+
+import concourse.mybir as mybir
+from concourse.masks import make_identity
+
+F32 = mybir.dt.float32
+BF16 = mybir.dt.bfloat16
+U32 = mybir.dt.uint32
+U8 = mybir.dt.uint8
+FP8X4 = mybir.dt.float8_e4m3fn_x4
+ALU = mybir.AluOpType
+ACT = mybir.ActivationFunctionType
+
+P = 128
+C = 256
+HEADS = 8
+HEAD_DIM = C // HEADS
+WINDOWS = 4
+TOKENS = 1024
+PAIR = 2
+SLICES = TOKENS // (PAIR * P)
+PASSES = 2
+PACK = 4
+HEADS_PER_LOAD = 4
+LOADS = SLICES * HEADS // HEADS_PER_LOAD
+GROUPS = LOADS * PAIR
+AHEAD = 4
+WEIGHT_BUFS = 4
+EPS = 1e-5
+
+FLOPS = 2 * HEADS * WINDOWS * TOKENS * TOKENS * HEAD_DIM
+
+
+def contraction_view(tokens_by_channels):
+    return tokens_by_channels.rearrange(
+        "b (wr g qh wc ql j) c -> (b wr) wc g qh ql (j c)", wr=2, g=PASSES, qh=16, wc=2, ql=8, j=PACK
+    )
+
+
+def output_view(tokens_by_channels):
+    return tokens_by_channels.rearrange(
+        "b (wr r wc pl a e) c -> (b wr) wc r pl a e c", wr=2, r=32, wc=2, pl=4, a=SLICES, e=PAIR
+    )
+
+
+def tile_swinmlpblocknew_pa_kernel(tc, x, norm1_w, norm1_b, spatial_w, spatial_b, out):
+    nc = tc.nc
+    x_by_t = contraction_view(x)
+    x_by_s = output_view(x)
+    out_by_s = output_view(out)
+
+    with ExitStack() as ctx:
+        keep = ctx.enter_context(tc.tile_pool(name="keep", bufs=1))
+        norm_pool = ctx.enter_context(tc.tile_pool(name="norm", bufs=3))
+        weight_pool = ctx.enter_context(tc.tile_pool(name="weights", bufs=WEIGHT_BUFS))
+        grouped_pool = ctx.enter_context(tc.tile_pool(name="grouped", bufs=AHEAD))
+        codes_pool = ctx.enter_context(tc.tile_pool(name="codes", bufs=3))
+        out_pool = ctx.enter_context(tc.tile_pool(name="outs", bufs=2))
+        psum_words = ctx.enter_context(tc.psum_pool(name="psum_words", bufs=6))
+        psum_acc = ctx.enter_context(tc.psum_pool(name="psum_acc", bufs=2))
+        ctx.enter_context(tc.manual_schedule())
+
+        x_sb = keep.tile([P, WINDOWS, SLICES, PAIR * C], BF16)
+        x_res = keep.tile([P, WINDOWS, SLICES, PAIR * C], BF16)
+        ident = keep.tile([P, P], F32)
+        ones = keep.tile([P, P], BF16)
+        norm_rows = keep.tile([P, 2 * C], BF16)
+        bias_bf = keep.tile([P, HEADS, SLICES * PAIR], BF16)
+        bias_col = keep.tile([P, HEADS, SLICES, PAIR], F32)
+        stats = keep.tile([P, WINDOWS, SLICES, 3 * PAIR], F32)
+        var_eps = keep.tile([P, WINDOWS, SLICES, PAIR], F32)
+        std = keep.tile([P, WINDOWS, SLICES, PAIR], F32)
+        rstd = keep.tile([P, WINDOWS, SLICES, PAIR], F32)
+        minus_mean_rstd = keep.tile([P, WINDOWS, SLICES, PAIR], F32)
+        xn_grouped = keep.tile([P, PASSES, HEADS, WINDOWS, HEAD_DIM * PACK], BF16, align_bytes=64)
+        x_codes = keep.tile([P, PASSES, HEADS * P], U32, align_bytes=64)
+        x_scales = keep.tile([P, PASSES, HEADS * P], U8, align_bytes=64)
+
+        normed = {}
+        w_raw = {}
+        words_ps = {}
+        w_grouped = {}
+        w_codes = {}
+        w_scales = {}
+        acc = {}
+        out_sb = {}
+
+        def statistics(n):
+            for a in range(SLICES):
+                nc.vector.bn_stats(
+                    out=stats[:, n, a, :], in_=x_sb[:, n, a, :].rearrange("q (e c) -> q c e", e=PAIR)
+                )
+            moments = stats[:, n, :, :].rearrange("q a (e k) -> q a e k", k=3)
+            nc.vector.tensor_scalar(
+                out=var_eps[:, n],
+                in0=moments[:, :, :, 2],
+                scalar1=1.0 / C,
+                scalar2=EPS,
+                op0=ALU.mult,
+                op1=ALU.add,
+            )
+            nc.scalar.sqrt(out=std[:, n], in_=var_eps[:, n])
+
+        def scales(n):
+            moments = stats[:, n, :, :].rearrange("q a (e k) -> q a e k", k=3)
+            nc.vector.reciprocal(out=rstd[:, n], in_=std[:, n])
+            nc.vector.scalar_tensor_tensor(
+                out=minus_mean_rstd[:, n],
+                in0=moments[:, :, :, 1],
+                scalar=-1.0,
+                in1=rstd[:, n],
+                op0=ALU.mult,
+                op1=ALU.mult,
+            )
+
+        def normalise(n):
+            normed_n = norm_pool.tile([P, SLICES * PAIR, C], F32, tag="normed")
+            normed[n] = normed_n
+            for a in range(SLICES):
+                for e in range(PAIR):
+                    nc.scalar.activation(
+                        out=normed_n[:, PAIR * a + e, :],
+                        in_=x_sb[:, n, a, e * C : (e + 1) * C],
+                        func=ACT.Identity,
+                        scale=rstd[:, n, a, e : e + 1],
+                        bias=minus_mean_rstd[:, n, a, e : e + 1],
+                    )
+
+        def gain_and_shift(n):
+            nc.vector.tensor_tensor(
+                out=normed[n][:],
+                in0=normed[n][:],
+                in1=norm_ps[:, 0:C].unsqueeze(1).to_broadcast([P, SLICES * PAIR, C]),
+                op=ALU.mult,
+            )
+            for g in range(PASSES):
+                nc.vector.tensor_tensor(
+                    out=xn_grouped[:, g, :, n, :].rearrange("q h (d j) -> q h d j", j=PACK),
+                    in0=normed[n][:, PACK * g : PACK * (g + 1), :].rearrange("q j (h d) -> q h d j", h=HEADS),
+                    in1=norm_ps[:, C : 2 * C]
+                    .rearrange("q (h d) -> q h d", h=HEADS)
+                    .unsqueeze(3)
+                    .to_broadcast([P, HEADS, HEAD_DIM, PACK]),
+                    op=ALU.add,
+                )
+
+        def load_weights(c):
+            a = c // 2
+            first_head = HEADS_PER_LOAD * (c % 2)
+            w_raw_c = weight_pool.tile([P, HEADS_PER_LOAD, PAIR, TOKENS], BF16, tag="w_raw")
+            w_raw[c] = w_raw_c
+            nc.sync.dma_start(
+                out=w_raw_c[:].rearrange("p i e t -> p i (e t)"),
+                in_=spatial_w[first_head : first_head + HEADS_PER_LOAD].rearrange(
+                    "i (p a e) t -> a p i (e t)", a=SLICES, e=PAIR
+                )[a],
+            )
+
+        def transpose_group(k):
+            for i in range(HEADS_PER_LOAD):
+                row_words = w_raw[k // PAIR][:, i, k % PAIR, :].bitcast(F32)
+                bank = psum_words.tile([P, SLICES, P], F32, tag="words")
+                words_ps[k, i] = bank
+                for g in range(PASSES):
+                    for u in range(2):
+                        nc.tensor.transpose(
+                            out=bank[:, 2 * g + u, :],
+                            in_=row_words[:, 2 * P * g + u : 2 * P * (g + 1) : 2],
+                            identity=ident[:],
+                        )
+
+        def copy_group_out(k):
+            grouped_k = grouped_pool.tile(
+                [P, HEADS_PER_LOAD, PASSES * P * PACK], BF16, tag="w_grouped", align_bytes=64
+            )
+            w_grouped[k] = grouped_k
+            for i in range(HEADS_PER_LOAD):
+                nc.scalar.copy(
+                    out=grouped_k[:, i, :].bitcast(F32).rearrange("q (g s u) -> q g s u", g=PASSES, u=2),
+                    in_=words_ps[k, i][:].rearrange("q (g u) s -> q g s u", g=PASSES),
+                )
+
+        def quantise_group(k):
+            codes_k = codes_pool.tile([P, HEADS_PER_LOAD, PASSES, P], U32, tag="w_codes", align_bytes=64)
+            scales_k = codes_pool.tile([P, HEADS_PER_LOAD, PASSES, P], U8, tag="w_scales", align_bytes=64)
+            w_codes[k] = codes_k
+            w_scales[k] = scales_k
+            nc.vector.quantize_mx(
+                out=codes_k[:].rearrange("q i g s -> q (i g s)").bitcast(FP8X4),
+                scales=scales_k[:].rearrange("q i g s -> q (i g s)"),
+                in_=w_grouped[k][:].rearrange("q i f -> q (i f)"),
+            )
+
+        def multiply_group(k):
+            first_head = HEADS_PER_LOAD * ((k // PAIR) % 2)
+            acc_k = psum_acc.tile([P, HEADS_PER_LOAD, P], F32, tag="acc")
+            acc[k] = acc_k
+            for i in range(HEADS_PER_LOAD):
+                h = first_head + i
+                for g in range(PASSES):
+                    nc.tensor.matmul_mx(
+                        out=acc_k[:, i, :],
+                        lhsT=w_codes[k][:, i, g, :].bitcast(FP8X4),
+                        lhsT_scale=w_scales[k][:, i, g, :],
+                        rhs=x_codes[:, g, h * P : (h + 1) * P].bitcast(FP8X4),
+                        rhs_scale=x_scales[:, g, h * P : (h + 1) * P],
+                        start=(g == 0),
+                        stop=(g == PASSES - 1),
+                    )
+
+        def finish_group(k):
+            a = k // (2 * PAIR)
+            e = k % PAIR
+            first_head = HEADS_PER_LOAD * ((k // PAIR) % 2)
+            if k % (2 * PAIR) == 0:
+                out_a = out_pool.tile([P, WINDOWS, PAIR, C], F32, tag="out_sb")
+                out_sb[a] = out_a
+            for i in range(HEADS_PER_LOAD):
+                h = first_head + i
+                nc.vector.scalar_tensor_tensor(
+                    out=out_sb[a][:, :, e, h * HEAD_DIM : (h + 1) * HEAD_DIM],
+                    in0=acc[k][:, i, :].rearrange("p (n d) -> p n d", n=WINDOWS),
+                    scalar=bias_col[:, h, a, e : e + 1],
+                    in1=x_res[:, :, a, e * C + h * HEAD_DIM : e * C + (h + 1) * HEAD_DIM],
+                    op0=ALU.add,
+                    op1=ALU.add,
+                )
+            if first_head + HEADS_PER_LOAD == HEADS:
+                for n in range(WINDOWS):
+                    nc.sync.dma_start(out=out_by_s[n // 2, n % 2, :, :, a, e, :], in_=out_sb[a][:, n, e, :])
+
+        def prepare_group(k):
+            transpose_group(k)
+            copy_group_out(k)
+            if k % PAIR == PAIR - 1 and k // PAIR + WEIGHT_BUFS < LOADS:
+                load_weights(k // PAIR + WEIGHT_BUFS)
+
+        for n in range(WINDOWS):
+            for g in range(PASSES):
+                nc.sync.dma_start(
+                    out=x_sb[:, n, 2 * g : 2 * g + 2, :].rearrange("p u f -> p (u f)"), in_=x_by_t[n // 2, n % 2, g]
+                )
+        for c in range(WEIGHT_BUFS):
+            load_weights(c)
+            if c == 1:
+                for n in range(WINDOWS):
+                    nc.sync.dma_start(
+                        out=x_res[:, n].rearrange("p a f -> p (a f)"),
+                        in_=x_by_s[n // 2, n % 2].rearrange("r pl a e c -> r pl (a e c)"),
+                    )
+
+        make_identity(nc, ident[:])
+        nc.vector.memset(norm_rows[:], 0.0)
+        nc.vector.memset(ones[:], 1.0)
+        nc.scalar.dma_start(out=norm_rows[0:1, 0:C], in_=norm1_w.unsqueeze(0))
+        nc.scalar.dma_start(out=norm_rows[0:1, C : 2 * C], in_=norm1_b.unsqueeze(0))
+        norm_ps = psum_acc.tile([P, 2 * C], F32, tag="acc")
+        nc.tensor.matmul(out=norm_ps[:], lhsT=ones[:], rhs=norm_rows[:], start=True, stop=True)
+        nc.scalar.dma_start(out=bias_bf[:], in_=spatial_b.rearrange("h (p i) -> p h i", i=SLICES * PAIR))
+
+        statistics(0)
+        for n in range(1, WINDOWS):
+            statistics(n)
+            scales(n - 1)
+            normalise(n - 1)
+        prepare_group(0)
+        gain_and_shift(0)
+        scales(WINDOWS - 1)
+        normalise(WINDOWS - 1)
+        for k in range(1, AHEAD):
+            prepare_group(k)
+        nc.scalar.copy(out=bias_col[:].rearrange("p h a e -> p h (a e)"), in_=bias_bf[:])
+        for n in range(1, WINDOWS):
+            gain_and_shift(n)
+        for g in range(PASSES):
+            nc.vector.quantize_mx(
+                out=x_codes[:, g, :].bitcast(FP8X4),
+                scales=x_scales[:, g, :],
+                in_=xn_grouped[:, g].rearrange("q h n f -> q (h n f)"),
+            )
+
+        for k in range(GROUPS):
+            quantise_group(k)
+            if k + AHEAD < GROUPS:
+                prepare_group(k + AHEAD)
+            multiply_group(k)
+            if k > 0:
+                finish_group(k - 1)
+        finish_group(GROUPS - 1)

@@ -17,64 +17,63 @@ HEADS = 8
 HEAD_DIM = C // HEADS
 WINDOWS = 4
 TOKENS = 1024
-PAIR = 2
-SLICES = TOKENS // (PAIR * P)
 PASSES = 2
 PACK = 4
-HEADS_PER_LOAD = 4
-LOADS = SLICES * HEADS // HEADS_PER_LOAD
-GROUPS = LOADS * PAIR
-AHEAD = 4
-WEIGHT_BUFS = 4
+PAIR = 2
+RUNS = PASSES * PACK
+HALVES = 2
+HALF = C // HALVES
+HEADS_PER_HALF = HEADS // HALVES
+QUARTERS = 4
+ITEMS = 2 * PAIR
+ORDER = [(quarter, 2 * half + i) for half in range(HALVES) for quarter in (0, 1) for i in range(2)] + [
+    (quarter, pair) for quarter in (2, 3) for pair in range(HEADS // 2)
+]
+GROUPS = len(ORDER)
+AHEAD = 8
+WEIGHT_BUFS = 6
 EPS = 1e-5
 
 FLOPS = 2 * HEADS * WINDOWS * TOKENS * TOKENS * HEAD_DIM
 
 
-def contraction_view(tokens_by_channels):
-    return tokens_by_channels.rearrange(
-        "b (wr g qh wc ql j) c -> (b wr) wc g qh ql (j c)", wr=2, g=PASSES, qh=16, wc=2, ql=8, j=PACK
-    )
-
-
-def output_view(tokens_by_channels):
-    return tokens_by_channels.rearrange(
-        "b (wr r wc pl a e) c -> (b wr) wc r pl a e c", wr=2, r=32, wc=2, pl=4, a=SLICES, e=PAIR
-    )
-
-
 def tile_swinmlpblocknew_pa_kernel(tc, x, norm1_w, norm1_b, spatial_w, spatial_b, out):
     nc = tc.nc
-    x_by_t = contraction_view(x)
-    x_by_s = output_view(x)
-    out_by_s = output_view(out)
+    x_by_t = x.rearrange(
+        "b (wr g row wc run j) c -> (b wr) wc g row run (j c)", wr=2, g=PASSES, row=16, wc=2, run=8, j=PACK
+    )
+    out_by_s = out.rearrange(
+        "b (wr g row wc run i e) c -> (b wr) wc g i row run (e c)", wr=2, g=PASSES, row=16, wc=2, run=8, i=2, e=PAIR
+    )
+    w_by_s = spatial_w.rearrange("h (g p i e) t -> h g i p (e t)", g=PASSES, p=P, i=2, e=PAIR)
 
     with ExitStack() as ctx:
         keep = ctx.enter_context(tc.tile_pool(name="keep", bufs=1))
-        norm_pool = ctx.enter_context(tc.tile_pool(name="norm", bufs=3))
+        norm_pool = ctx.enter_context(tc.tile_pool(name="norm", bufs=WINDOWS))
         weight_pool = ctx.enter_context(tc.tile_pool(name="weights", bufs=WEIGHT_BUFS))
         grouped_pool = ctx.enter_context(tc.tile_pool(name="grouped", bufs=AHEAD))
         codes_pool = ctx.enter_context(tc.tile_pool(name="codes", bufs=3))
         out_pool = ctx.enter_context(tc.tile_pool(name="outs", bufs=2))
-        psum_words = ctx.enter_context(tc.psum_pool(name="psum_words", bufs=6))
+        psum_words = ctx.enter_context(tc.psum_pool(name="psum_words", bufs=5))
         psum_acc = ctx.enter_context(tc.psum_pool(name="psum_acc", bufs=2))
+        psum_norm = ctx.enter_context(tc.psum_pool(name="psum_norm", bufs=1))
         ctx.enter_context(tc.manual_schedule())
 
-        x_sb = keep.tile([P, WINDOWS, SLICES, PAIR * C], BF16)
-        x_res = keep.tile([P, WINDOWS, SLICES, PAIR * C], BF16)
+        x_sb = keep.tile([P, WINDOWS, RUNS, C], BF16)
         ident = keep.tile([P, P], F32)
         ones = keep.tile([P, P], BF16)
         norm_rows = keep.tile([P, 2 * C], BF16)
-        bias_bf = keep.tile([P, HEADS, SLICES * PAIR], BF16)
-        bias_col = keep.tile([P, HEADS, SLICES, PAIR], F32)
-        stats = keep.tile([P, WINDOWS, SLICES, 3 * PAIR], F32)
-        var_eps = keep.tile([P, WINDOWS, SLICES, PAIR], F32)
-        std = keep.tile([P, WINDOWS, SLICES, PAIR], F32)
-        rstd = keep.tile([P, WINDOWS, SLICES, PAIR], F32)
-        minus_mean_rstd = keep.tile([P, WINDOWS, SLICES, PAIR], F32)
-        xn_grouped = keep.tile([P, PASSES, HEADS, WINDOWS, HEAD_DIM * PACK], BF16, align_bytes=64)
-        x_codes = keep.tile([P, PASSES, HEADS * P], U32, align_bytes=64)
-        x_scales = keep.tile([P, PASSES, HEADS * P], U8, align_bytes=64)
+        norm_sb = keep.tile([P, 2 * C], F32)
+        scratch = keep.tile([P, 1], F32)
+        bias_rows = keep.tile([P, PASSES * P * PACK // PASSES], BF16)
+        bias_col = keep.tile([P, PACK, HEADS * PASSES], F32)
+        stats = keep.tile([P, WINDOWS, RUNS // PAIR, 3 * PAIR], F32)
+        var_eps = keep.tile([P, WINDOWS, RUNS], F32)
+        rstd = keep.tile([P, WINDOWS, RUNS], F32)
+        std = keep.tile([P, WINDOWS, RUNS], F32)
+        xn_grouped = keep.tile([P, HALVES, PASSES, HEADS_PER_HALF, WINDOWS, HEAD_DIM * PACK], BF16, align_bytes=64)
+        x_codes = keep.tile([P, HALVES, PASSES, HEADS_PER_HALF, P], U32, align_bytes=64)
+        x_scales = keep.tile([P, HALVES, PASSES, HEADS_PER_HALF, P], U8, align_bytes=64)
 
         normed = {}
         w_raw = {}
@@ -85,82 +84,83 @@ def tile_swinmlpblocknew_pa_kernel(tc, x, norm1_w, norm1_b, spatial_w, spatial_b
         acc = {}
         out_sb = {}
 
-        def statistics(n):
-            for a in range(SLICES):
-                nc.vector.bn_stats(
-                    out=stats[:, n, a, :], in_=x_sb[:, n, a, :].rearrange("q (e c) -> q c e", e=PAIR)
-                )
-            moments = stats[:, n, :, :].rearrange("q a (e k) -> q a e k", k=3)
-            nc.vector.tensor_scalar(
-                out=var_eps[:, n],
-                in0=moments[:, :, :, 2],
-                scalar1=1.0 / C,
-                scalar2=EPS,
-                op0=ALU.mult,
-                op1=ALU.add,
-            )
-            nc.scalar.sqrt(out=std[:, n], in_=var_eps[:, n])
+        def moments(n, k):
+            return stats[:, n, :, :].rearrange("q a (e k) -> q a e k", k=3)[:, :, :, k]
 
-        def scales(n):
-            moments = stats[:, n, :, :].rearrange("q a (e k) -> q a e k", k=3)
-            nc.vector.reciprocal(out=rstd[:, n], in_=std[:, n])
-            nc.vector.scalar_tensor_tensor(
-                out=minus_mean_rstd[:, n],
-                in0=moments[:, :, :, 1],
-                scalar=-1.0,
-                in1=rstd[:, n],
-                op0=ALU.mult,
-                op1=ALU.mult,
+        def pairs(values, n):
+            return values[:, n, :].rearrange("q (a e) -> q a e", e=PAIR)
+
+        def statistics(n):
+            for a in range(RUNS // PAIR):
+                nc.vector.bn_stats(
+                    out=stats[:, n, a, :],
+                    in_=x_sb[:, n, PAIR * a : PAIR * (a + 1), :].rearrange("q e c -> q c e"),
+                )
+            nc.vector.tensor_scalar(
+                out=pairs(var_eps, n), in0=moments(n, 2), scalar1=1.0 / C, scalar2=EPS, op0=ALU.mult, op1=ALU.add
             )
+
+        def deviation(n):
+            nc.scalar.sqrt(out=std[:, n, :], in_=var_eps[:, n, :])
 
         def normalise(n):
-            normed_n = norm_pool.tile([P, SLICES * PAIR, C], F32, tag="normed")
+            nc.vector.reciprocal(out=rstd[:, n, :], in_=std[:, n, :])
+            normed_n = norm_pool.tile([P, RUNS, C], F32, tag="normed")
             normed[n] = normed_n
-            for a in range(SLICES):
-                for e in range(PAIR):
-                    nc.scalar.activation(
-                        out=normed_n[:, PAIR * a + e, :],
-                        in_=x_sb[:, n, a, e * C : (e + 1) * C],
-                        func=ACT.Identity,
-                        scale=rstd[:, n, a, e : e + 1],
-                        bias=minus_mean_rstd[:, n, a, e : e + 1],
-                    )
+            for r in range(RUNS):
+                nc.vector.tensor_scalar(
+                    out=normed_n[:, r, :],
+                    in0=x_sb[:, n, r, :],
+                    scalar1=stats[:, n, r // PAIR, 3 * (r % PAIR) + 1 : 3 * (r % PAIR) + 2],
+                    scalar2=rstd[:, n, r : r + 1],
+                    op0=ALU.subtract,
+                    op1=ALU.mult,
+                )
 
-        def gain_and_shift(n):
-            nc.vector.tensor_tensor(
-                out=normed[n][:],
-                in0=normed[n][:],
-                in1=norm_ps[:, 0:C].unsqueeze(1).to_broadcast([P, SLICES * PAIR, C]),
+        def gain(n, half):
+            cols = slice(half * HALF, (half + 1) * HALF)
+            nc.gpsimd.tensor_tensor(
+                out=normed[n][:, :, cols],
+                in0=normed[n][:, :, cols],
+                in1=norm_sb[:, cols].unsqueeze(1).to_broadcast([P, RUNS, HALF]),
                 op=ALU.mult,
             )
+
+        def shift(n, half):
+            cols = slice(half * HALF, (half + 1) * HALF)
             for g in range(PASSES):
                 nc.vector.tensor_tensor(
-                    out=xn_grouped[:, g, :, n, :].rearrange("q h (d j) -> q h d j", j=PACK),
-                    in0=normed[n][:, PACK * g : PACK * (g + 1), :].rearrange("q j (h d) -> q h d j", h=HEADS),
-                    in1=norm_ps[:, C : 2 * C]
-                    .rearrange("q (h d) -> q h d", h=HEADS)
+                    out=xn_grouped[:, half, g, :, n, :].rearrange("q h (d j) -> q h d j", j=PACK),
+                    in0=normed[n][:, PACK * g : PACK * (g + 1), cols].rearrange("q j (h d) -> q h d j", h=HEADS_PER_HALF),
+                    in1=norm_ps[:, C + half * HALF : C + (half + 1) * HALF]
+                    .rearrange("q (h d) -> q h d", h=HEADS_PER_HALF)
                     .unsqueeze(3)
-                    .to_broadcast([P, HEADS, HEAD_DIM, PACK]),
+                    .to_broadcast([P, HEADS_PER_HALF, HEAD_DIM, PACK]),
                     op=ALU.add,
                 )
 
-        def load_weights(c):
-            a = c // 2
-            first_head = HEADS_PER_LOAD * (c % 2)
-            w_raw_c = weight_pool.tile([P, HEADS_PER_LOAD, PAIR, TOKENS], BF16, tag="w_raw")
-            w_raw[c] = w_raw_c
-            nc.sync.dma_start(
-                out=w_raw_c[:].rearrange("p i e t -> p i (e t)"),
-                in_=spatial_w[first_head : first_head + HEADS_PER_LOAD].rearrange(
-                    "i (p a e) t -> a p i (e t)", a=SLICES, e=PAIR
-                )[a],
+        def quantise_x(half):
+            nc.vector.quantize_mx(
+                out=x_codes[:, half].rearrange("q g h f -> q (g h f)").bitcast(FP8X4),
+                scales=x_scales[:, half].rearrange("q g h f -> q (g h f)"),
+                in_=xn_grouped[:, half].rearrange("q g h n f -> q (g h n f)"),
             )
 
-        def transpose_group(k):
-            for i in range(HEADS_PER_LOAD):
-                row_words = w_raw[k // PAIR][:, i, k % PAIR, :].bitcast(F32)
-                bank = psum_words.tile([P, SLICES, P], F32, tag="words")
-                words_ps[k, i] = bank
+        def load_weights(k, head):
+            quarter, heads = ORDER[k]
+            if head == 0:
+                w_raw_k = weight_pool.tile([P, 2, PAIR, TOKENS], BF16, tag="w_raw")
+                w_raw[k] = w_raw_k
+            nc.sync.dma_start(
+                out=w_raw[k][:, head].rearrange("p e t -> p (e t)"),
+                in_=w_by_s[2 * heads + head, quarter // 2, quarter % 2],
+            )
+
+        def transpose_items(k, items):
+            for item in items:
+                row_words = w_raw[k][:, item // PAIR, item % PAIR, :].bitcast(F32)
+                bank = psum_words.tile([P, 2 * PASSES, P], F32, tag="words")
+                words_ps[k, item] = bank
                 for g in range(PASSES):
                     for u in range(2):
                         nc.tensor.transpose(
@@ -169,20 +169,29 @@ def tile_swinmlpblocknew_pa_kernel(tc, x, norm1_w, norm1_b, spatial_w, spatial_b
                             identity=ident[:],
                         )
 
-        def copy_group_out(k):
-            grouped_k = grouped_pool.tile(
-                [P, HEADS_PER_LOAD, PASSES * P * PACK], BF16, tag="w_grouped", align_bytes=64
-            )
-            w_grouped[k] = grouped_k
-            for i in range(HEADS_PER_LOAD):
+        def copy_items_out(k, items):
+            if k not in w_grouped:
+                grouped_k = grouped_pool.tile([P, ITEMS, PASSES * P * PACK], BF16, tag="w_grouped", align_bytes=64)
+                w_grouped[k] = grouped_k
+            for item in items:
                 nc.scalar.copy(
-                    out=grouped_k[:, i, :].bitcast(F32).rearrange("q (g s u) -> q g s u", g=PASSES, u=2),
-                    in_=words_ps[k, i][:].rearrange("q (g u) s -> q g s u", g=PASSES),
+                    out=w_grouped[k][:, item, :].bitcast(F32).rearrange("q (g s u) -> q g s u", g=PASSES, u=2),
+                    in_=words_ps[k, item][:].rearrange("q (g u) s -> q g s u", g=PASSES),
                 )
 
+        def load_next(k):
+            if k + WEIGHT_BUFS < GROUPS:
+                load_weights(k + WEIGHT_BUFS, 0)
+                load_weights(k + WEIGHT_BUFS, 1)
+
+        def prepare_group(k):
+            transpose_items(k, range(ITEMS))
+            load_next(k)
+            copy_items_out(k, range(ITEMS))
+
         def quantise_group(k):
-            codes_k = codes_pool.tile([P, HEADS_PER_LOAD, PASSES, P], U32, tag="w_codes", align_bytes=64)
-            scales_k = codes_pool.tile([P, HEADS_PER_LOAD, PASSES, P], U8, tag="w_scales", align_bytes=64)
+            codes_k = codes_pool.tile([P, ITEMS, PASSES, P], U32, tag="w_codes", align_bytes=64)
+            scales_k = codes_pool.tile([P, ITEMS, PASSES, P], U8, tag="w_scales", align_bytes=64)
             w_codes[k] = codes_k
             w_scales[k] = scales_k
             nc.vector.quantize_mx(
@@ -192,98 +201,135 @@ def tile_swinmlpblocknew_pa_kernel(tc, x, norm1_w, norm1_b, spatial_w, spatial_b
             )
 
         def multiply_group(k):
-            first_head = HEADS_PER_LOAD * ((k // PAIR) % 2)
-            acc_k = psum_acc.tile([P, HEADS_PER_LOAD, P], F32, tag="acc")
+            quarter, heads = ORDER[k]
+            acc_k = psum_acc.tile([P, ITEMS, P], F32, tag="acc")
             acc[k] = acc_k
-            for i in range(HEADS_PER_LOAD):
-                h = first_head + i
+            for item in range(ITEMS):
+                h = 2 * heads + item // PAIR
+                half = h // HEADS_PER_HALF
                 for g in range(PASSES):
                     nc.tensor.matmul_mx(
-                        out=acc_k[:, i, :],
-                        lhsT=w_codes[k][:, i, g, :].bitcast(FP8X4),
-                        lhsT_scale=w_scales[k][:, i, g, :],
-                        rhs=x_codes[:, g, h * P : (h + 1) * P].bitcast(FP8X4),
-                        rhs_scale=x_scales[:, g, h * P : (h + 1) * P],
+                        out=acc_k[:, item, :],
+                        lhsT=w_codes[k][:, item, g, :].bitcast(FP8X4),
+                        lhsT_scale=w_scales[k][:, item, g, :],
+                        rhs=x_codes[:, half, g, h % HEADS_PER_HALF, :].bitcast(FP8X4),
+                        rhs_scale=x_scales[:, half, g, h % HEADS_PER_HALF, :],
                         start=(g == 0),
                         stop=(g == PASSES - 1),
                     )
 
         def finish_group(k):
-            a = k // (2 * PAIR)
-            e = k % PAIR
-            first_head = HEADS_PER_LOAD * ((k // PAIR) % 2)
-            if k % (2 * PAIR) == 0:
-                out_a = out_pool.tile([P, WINDOWS, PAIR, C], F32, tag="out_sb")
-                out_sb[a] = out_a
-            for i in range(HEADS_PER_LOAD):
-                h = first_head + i
+            quarter, heads = ORDER[k]
+            g = quarter // 2
+            if heads == 0:
+                out_q = out_pool.tile([P, WINDOWS, PAIR, C], F32, tag="out_sb")
+                out_sb[quarter] = out_q
+            for item in range(ITEMS):
+                h = 2 * heads + item // PAIR
+                e = item % PAIR
+                j = PAIR * (quarter % 2) + e
+                cols = slice(h * HEAD_DIM, (h + 1) * HEAD_DIM)
                 nc.vector.scalar_tensor_tensor(
-                    out=out_sb[a][:, :, e, h * HEAD_DIM : (h + 1) * HEAD_DIM],
-                    in0=acc[k][:, i, :].rearrange("p (n d) -> p n d", n=WINDOWS),
-                    scalar=bias_col[:, h, a, e : e + 1],
-                    in1=x_res[:, :, a, e * C + h * HEAD_DIM : e * C + (h + 1) * HEAD_DIM],
+                    out=out_sb[quarter][:, :, e, cols],
+                    in0=acc[k][:, item, :].rearrange("p (n d) -> p n d", n=WINDOWS),
+                    scalar=bias_col[:, j, PASSES * h + g : PASSES * h + g + 1],
+                    in1=x_sb[:, :, PACK * g + j, cols],
                     op0=ALU.add,
                     op1=ALU.add,
                 )
-            if first_head + HEADS_PER_LOAD == HEADS:
-                for n in range(WINDOWS):
-                    nc.sync.dma_start(out=out_by_s[n // 2, n % 2, :, :, a, e, :], in_=out_sb[a][:, n, e, :])
-
-        def prepare_group(k):
-            transpose_group(k)
-            copy_group_out(k)
-            if k % PAIR == PAIR - 1 and k // PAIR + WEIGHT_BUFS < LOADS:
-                load_weights(k // PAIR + WEIGHT_BUFS)
-
-        for n in range(WINDOWS):
-            for g in range(PASSES):
-                nc.sync.dma_start(
-                    out=x_sb[:, n, 2 * g : 2 * g + 2, :].rearrange("p u f -> p (u f)"), in_=x_by_t[n // 2, n % 2, g]
-                )
-        for c in range(WEIGHT_BUFS):
-            load_weights(c)
-            if c == 1:
+            if heads == HEADS // 2 - 1:
                 for n in range(WINDOWS):
                     nc.sync.dma_start(
-                        out=x_res[:, n].rearrange("p a f -> p (a f)"),
-                        in_=x_by_s[n // 2, n % 2].rearrange("r pl a e c -> r pl (a e c)"),
+                        out=out_by_s[n // 2, n % 2, g, quarter % 2],
+                        in_=out_sb[quarter][:, n].rearrange("p e c -> p (e c)"),
                     )
 
+        def load_x(n):
+            for g in range(PASSES):
+                nc.sync.dma_start(
+                    out=x_sb[:, n, PACK * g : PACK * (g + 1), :].rearrange("q j c -> q (j c)"),
+                    in_=x_by_t[n // 2, n % 2, g],
+                )
+
+        load_x(0)
+        load_x(1)
+        load_weights(0, 0)
+        load_weights(0, 1)
+        load_x(2)
+        load_weights(1, 0)
+        load_x(3)
+        load_weights(1, 1)
+        for k in range(2, WEIGHT_BUFS):
+            load_weights(k, 0)
+            load_weights(k, 1)
+
         make_identity(nc, ident[:])
-        nc.vector.memset(norm_rows[:], 0.0)
         nc.vector.memset(ones[:], 1.0)
+        nc.vector.memset(norm_rows[:], 0.0)
+        nc.gpsimd.memset(bias_rows[:], 0.0)
+        nc.scalar.sqrt(out=scratch[:], in_=ones[:, 0:1])
         nc.scalar.dma_start(out=norm_rows[0:1, 0:C], in_=norm1_w.unsqueeze(0))
         nc.scalar.dma_start(out=norm_rows[0:1, C : 2 * C], in_=norm1_b.unsqueeze(0))
-        norm_ps = psum_acc.tile([P, 2 * C], F32, tag="acc")
-        nc.tensor.matmul(out=norm_ps[:], lhsT=ones[:], rhs=norm_rows[:], start=True, stop=True)
-        nc.scalar.dma_start(out=bias_bf[:], in_=spatial_b.rearrange("h (p i) -> p h i", i=SLICES * PAIR))
-
+        nc.scalar.dma_start(
+            out=bias_rows[0 : HEADS * PASSES, :], in_=spatial_b.rearrange("h (g k) -> (h g) k", g=PASSES)
+        )
         statistics(0)
-        for n in range(1, WINDOWS):
-            statistics(n)
-            scales(n - 1)
-            normalise(n - 1)
-        prepare_group(0)
-        gain_and_shift(0)
-        scales(WINDOWS - 1)
-        normalise(WINDOWS - 1)
-        for k in range(1, AHEAD):
+        deviation(0)
+        transpose_items(0, range(2))
+        copy_items_out(0, range(2))
+        norm_ps = psum_norm.tile([P, 2 * C], F32, tag="norm")
+        nc.tensor.matmul(out=norm_ps[:], lhsT=ones[:], rhs=norm_rows[:], start=True, stop=True)
+        nc.scalar.copy(out=norm_sb[:], in_=norm_ps[:])
+        statistics(1)
+        deviation(1)
+        normalise(0)
+        gain(0, 0)
+        transpose_items(0, range(2, ITEMS))
+        load_next(0)
+        copy_items_out(0, range(2, ITEMS))
+        transpose_items(1, range(ITEMS))
+        load_next(1)
+        copy_items_out(1, range(2))
+        statistics(2)
+        deviation(2)
+        normalise(1)
+        gain(1, 0)
+        copy_items_out(1, range(2, ITEMS))
+        prepare_group(2)
+        statistics(3)
+        deviation(3)
+        normalise(2)
+        gain(2, 0)
+        normalise(3)
+        gain(3, 0)
+        for k in range(3, AHEAD):
             prepare_group(k)
-        nc.scalar.copy(out=bias_col[:].rearrange("p h a e -> p h (a e)"), in_=bias_bf[:])
-        for n in range(1, WINDOWS):
-            gain_and_shift(n)
-        for g in range(PASSES):
-            nc.vector.quantize_mx(
-                out=x_codes[:, g, :].bitcast(FP8X4),
-                scales=x_scales[:, g, :],
-                in_=xn_grouped[:, g].rearrange("q h n f -> q (h n f)"),
+        bias_ps = psum_words.tile([P, 2 * PASSES, P], F32, tag="words")
+        for u in range(2):
+            nc.tensor.transpose(out=bias_ps[:, u, :], in_=bias_rows[:].bitcast(F32)[:, u : 2 * P : 2], identity=ident[:])
+        for u in range(2):
+            nc.scalar.copy(
+                out=bias_col[:, PAIR * u : PAIR * (u + 1), :],
+                in_=bias_ps[:, u, 0 : HEADS * PASSES].bitcast(BF16).rearrange("p (r e) -> p e r", e=PAIR),
             )
+        shift(0, 0)
+        shift(1, 0)
+        quantise_group(0)
+        shift(2, 0)
+        shift(3, 0)
+        quantise_x(0)
+        for n in range(WINDOWS):
+            gain(n, 1)
 
         for k in range(GROUPS):
-            quantise_group(k)
+            if k > 0:
+                quantise_group(k)
+                finish_group(k - 1)
+            if 0 < k <= WINDOWS:
+                shift(k - 1, 1)
+            if k == WINDOWS:
+                quantise_x(1)
             if k + AHEAD < GROUPS:
                 prepare_group(k + AHEAD)
             multiply_group(k)
-            if k > 0:
-                finish_group(k - 1)
         finish_group(GROUPS - 1)

@@ -21,16 +21,17 @@ PASSES = 2
 PACK = 4
 PAIR = 2
 RUNS = PASSES * PACK
-HALVES = 2
-HALF = C // HALVES
-HEADS_PER_HALF = HEADS // HALVES
+PAIRS = 4
+PAIR_CH = C // PAIRS
+HEADS_PER_PAIR = HEADS // PAIRS
 QUARTERS = 4
-ITEMS = 2 * PAIR
-ORDER = [(quarter, 2 * half + i) for half in range(HALVES) for quarter in (0, 1) for i in range(2)] + [
-    (quarter, pair) for quarter in (2, 3) for pair in range(HEADS // 2)
+ITEMS = HEADS_PER_PAIR * PAIR
+ORDER = [(pair, quarter) for pair in range(PAIRS) for quarter in range(QUARTERS - 1)] + [
+    (pair, QUARTERS - 1) for pair in range(PAIRS)
 ]
 GROUPS = len(ORDER)
-AHEAD = 8
+AHEAD = 5
+LEAD = 4
 WEIGHT_BUFS = 6
 EPS = 1e-5
 
@@ -49,11 +50,11 @@ def tile_swinmlpblocknew_pa_kernel(tc, x, norm1_w, norm1_b, spatial_w, spatial_b
 
     with ExitStack() as ctx:
         keep = ctx.enter_context(tc.tile_pool(name="keep", bufs=1))
-        norm_pool = ctx.enter_context(tc.tile_pool(name="norm", bufs=WINDOWS))
+        norm_pool = ctx.enter_context(tc.tile_pool(name="norm", bufs=2))
         weight_pool = ctx.enter_context(tc.tile_pool(name="weights", bufs=WEIGHT_BUFS))
         grouped_pool = ctx.enter_context(tc.tile_pool(name="grouped", bufs=AHEAD))
-        codes_pool = ctx.enter_context(tc.tile_pool(name="codes", bufs=3))
-        out_pool = ctx.enter_context(tc.tile_pool(name="outs", bufs=2))
+        codes_pool = ctx.enter_context(tc.tile_pool(name="codes", bufs=LEAD + 3))
+        out_pool = ctx.enter_context(tc.tile_pool(name="outs", bufs=QUARTERS))
         psum_words = ctx.enter_context(tc.psum_pool(name="psum_words", bufs=5))
         psum_acc = ctx.enter_context(tc.psum_pool(name="psum_acc", bufs=2))
         psum_norm = ctx.enter_context(tc.psum_pool(name="psum_norm", bufs=1))
@@ -63,19 +64,20 @@ def tile_swinmlpblocknew_pa_kernel(tc, x, norm1_w, norm1_b, spatial_w, spatial_b
         ident = keep.tile([P, P], F32)
         ones = keep.tile([P, P], BF16)
         norm_rows = keep.tile([P, 2 * C], BF16)
-        norm_sb = keep.tile([P, 2 * C], F32)
         scratch = keep.tile([P, 1], F32)
         bias_rows = keep.tile([P, PASSES * P * PACK // PASSES], BF16)
         bias_col = keep.tile([P, PACK, HEADS * PASSES], F32)
         stats = keep.tile([P, WINDOWS, RUNS // PAIR, 3 * PAIR], F32)
-        var_eps = keep.tile([P, WINDOWS, RUNS], F32)
+        eps_col = keep.tile([P, 1], F32)
         rstd = keep.tile([P, WINDOWS, RUNS], F32)
         std = keep.tile([P, WINDOWS, RUNS], F32)
-        xn_grouped = keep.tile([P, HALVES, PASSES, HEADS_PER_HALF, WINDOWS, HEAD_DIM * PACK], BF16, align_bytes=64)
-        x_codes = keep.tile([P, HALVES, PASSES, HEADS_PER_HALF, P], U32, align_bytes=64)
-        x_scales = keep.tile([P, HALVES, PASSES, HEADS_PER_HALF, P], U8, align_bytes=64)
+        minus_mean_rstd = keep.tile([P, WINDOWS, RUNS], F32)
+        norm_sb = keep.tile([P, 2 * C], F32)
+        x_codes = keep.tile([P, PAIRS, PASSES, HEADS_PER_PAIR, P], U32, align_bytes=64)
+        x_scales = keep.tile([P, PAIRS, PASSES, HEADS_PER_PAIR, P], U8, align_bytes=64)
 
         normed = {}
+        xn_grouped = {}
         w_raw = {}
         words_ps = {}
         w_grouped = {}
@@ -90,64 +92,75 @@ def tile_swinmlpblocknew_pa_kernel(tc, x, norm1_w, norm1_b, spatial_w, spatial_b
         def pairs(values, n):
             return values[:, n, :].rearrange("q (a e) -> q a e", e=PAIR)
 
-        def statistics(n):
-            for a in range(RUNS // PAIR):
+        def statistics(n, pairs_of_tokens):
+            for a in pairs_of_tokens:
                 nc.vector.bn_stats(
                     out=stats[:, n, a, :],
                     in_=x_sb[:, n, PAIR * a : PAIR * (a + 1), :].rearrange("q e c -> q c e"),
                 )
-            nc.vector.tensor_scalar(
-                out=pairs(var_eps, n), in0=moments(n, 2), scalar1=1.0 / C, scalar2=EPS, op0=ALU.mult, op1=ALU.add
-            )
 
         def deviation(n):
-            nc.scalar.sqrt(out=std[:, n, :], in_=var_eps[:, n, :])
+            nc.scalar.activation(out=pairs(std, n), in_=moments(n, 2), func=ACT.Sqrt, scale=1.0 / C, bias=eps_col[:])
 
-        def normalise(n):
+        def inverse(n):
             nc.vector.reciprocal(out=rstd[:, n, :], in_=std[:, n, :])
-            normed_n = norm_pool.tile([P, RUNS, C], F32, tag="normed")
-            normed[n] = normed_n
+
+        def offset(n):
+            nc.vector.scalar_tensor_tensor(
+                out=pairs(minus_mean_rstd, n),
+                in0=moments(n, 1),
+                scalar=-1.0,
+                in1=pairs(rstd, n),
+                op0=ALU.mult,
+                op1=ALU.mult,
+            )
+
+        def normalise(n, pair):
+            if n == 0:
+                normed_p = norm_pool.tile([P, WINDOWS, RUNS, PAIR_CH], F32, tag="normed")
+                grouped_p = norm_pool.tile(
+                    [P, PASSES, HEADS_PER_PAIR, WINDOWS, HEAD_DIM * PACK], BF16, tag="xn_grouped", align_bytes=64
+                )
+                normed[pair] = normed_p
+                xn_grouped[pair] = grouped_p
             for r in range(RUNS):
-                nc.vector.tensor_scalar(
-                    out=normed_n[:, r, :],
-                    in0=x_sb[:, n, r, :],
-                    scalar1=stats[:, n, r // PAIR, 3 * (r % PAIR) + 1 : 3 * (r % PAIR) + 2],
-                    scalar2=rstd[:, n, r : r + 1],
-                    op0=ALU.subtract,
-                    op1=ALU.mult,
+                nc.scalar.activation(
+                    out=normed[pair][:, n, r, :],
+                    in_=x_sb[:, n, r, pair * PAIR_CH : (pair + 1) * PAIR_CH],
+                    func=ACT.Identity,
+                    scale=rstd[:, n, r : r + 1],
+                    bias=minus_mean_rstd[:, n, r : r + 1],
                 )
 
-        def gain(n, half):
-            cols = slice(half * HALF, (half + 1) * HALF)
+        def gain(n, pair):
             nc.gpsimd.tensor_tensor(
-                out=normed[n][:, :, cols],
-                in0=normed[n][:, :, cols],
-                in1=norm_sb[:, cols].unsqueeze(1).to_broadcast([P, RUNS, HALF]),
+                out=normed[pair][:, n],
+                in0=normed[pair][:, n],
+                in1=norm_sb[:, pair * PAIR_CH : (pair + 1) * PAIR_CH].unsqueeze(1).to_broadcast([P, RUNS, PAIR_CH]),
                 op=ALU.mult,
             )
 
-        def shift(n, half):
-            cols = slice(half * HALF, (half + 1) * HALF)
+        def shift(n, pair):
             for g in range(PASSES):
                 nc.vector.tensor_tensor(
-                    out=xn_grouped[:, half, g, :, n, :].rearrange("q h (d j) -> q h d j", j=PACK),
-                    in0=normed[n][:, PACK * g : PACK * (g + 1), cols].rearrange("q j (h d) -> q h d j", h=HEADS_PER_HALF),
-                    in1=norm_ps[:, C + half * HALF : C + (half + 1) * HALF]
-                    .rearrange("q (h d) -> q h d", h=HEADS_PER_HALF)
+                    out=xn_grouped[pair][:, g, :, n, :].rearrange("q h (d j) -> q h d j", j=PACK),
+                    in0=normed[pair][:, n, PACK * g : PACK * (g + 1), :].rearrange("q j (h d) -> q h d j", h=HEADS_PER_PAIR),
+                    in1=norm_ps[:, C + pair * PAIR_CH : C + (pair + 1) * PAIR_CH]
+                    .rearrange("q (h d) -> q h d", h=HEADS_PER_PAIR)
                     .unsqueeze(3)
-                    .to_broadcast([P, HEADS_PER_HALF, HEAD_DIM, PACK]),
+                    .to_broadcast([P, HEADS_PER_PAIR, HEAD_DIM, PACK]),
                     op=ALU.add,
                 )
 
-        def quantise_x(half):
+        def quantise_x(pair):
             nc.vector.quantize_mx(
-                out=x_codes[:, half].rearrange("q g h f -> q (g h f)").bitcast(FP8X4),
-                scales=x_scales[:, half].rearrange("q g h f -> q (g h f)"),
-                in_=xn_grouped[:, half].rearrange("q g h n f -> q (g h n f)"),
+                out=x_codes[:, pair].rearrange("q g h f -> q (g h f)").bitcast(FP8X4),
+                scales=x_scales[:, pair].rearrange("q g h f -> q (g h f)"),
+                in_=xn_grouped[pair][:].rearrange("q g h n f -> q (g h n f)"),
             )
 
         def load_weights(k, head):
-            quarter, heads = ORDER[k]
+            heads, quarter = ORDER[k]
             if head == 0:
                 w_raw_k = weight_pool.tile([P, 2, PAIR, TOKENS], BF16, tag="w_raw")
                 w_raw[k] = w_raw_k
@@ -201,31 +214,29 @@ def tile_swinmlpblocknew_pa_kernel(tc, x, norm1_w, norm1_b, spatial_w, spatial_b
             )
 
         def multiply_group(k):
-            quarter, heads = ORDER[k]
+            heads, quarter = ORDER[k]
             acc_k = psum_acc.tile([P, ITEMS, P], F32, tag="acc")
             acc[k] = acc_k
             for item in range(ITEMS):
-                h = 2 * heads + item // PAIR
-                half = h // HEADS_PER_HALF
                 for g in range(PASSES):
                     nc.tensor.matmul_mx(
                         out=acc_k[:, item, :],
                         lhsT=w_codes[k][:, item, g, :].bitcast(FP8X4),
                         lhsT_scale=w_scales[k][:, item, g, :],
-                        rhs=x_codes[:, half, g, h % HEADS_PER_HALF, :].bitcast(FP8X4),
-                        rhs_scale=x_scales[:, half, g, h % HEADS_PER_HALF, :],
+                        rhs=x_codes[:, heads, g, item // PAIR, :].bitcast(FP8X4),
+                        rhs_scale=x_scales[:, heads, g, item // PAIR, :],
                         start=(g == 0),
                         stop=(g == PASSES - 1),
                     )
 
         def finish_group(k):
-            quarter, heads = ORDER[k]
+            heads, quarter = ORDER[k]
             g = quarter // 2
             if heads == 0:
                 out_q = out_pool.tile([P, WINDOWS, PAIR, C], F32, tag="out_sb")
                 out_sb[quarter] = out_q
             for item in range(ITEMS):
-                h = 2 * heads + item // PAIR
+                h = HEADS_PER_PAIR * heads + item // PAIR
                 e = item % PAIR
                 j = PAIR * (quarter % 2) + e
                 cols = slice(h * HEAD_DIM, (h + 1) * HEAD_DIM)
@@ -237,10 +248,10 @@ def tile_swinmlpblocknew_pa_kernel(tc, x, norm1_w, norm1_b, spatial_w, spatial_b
                     op0=ALU.add,
                     op1=ALU.add,
                 )
-            if heads == HEADS // 2 - 1:
+            if heads == PAIRS - 1:
                 for n in range(WINDOWS):
                     nc.sync.dma_start(
-                        out=out_by_s[n // 2, n % 2, g, quarter % 2],
+                        out=out_by_s[n // 2, n % 2, quarter // 2, quarter % 2],
                         in_=out_sb[quarter][:, n].rearrange("p e c -> p (e c)"),
                     )
 
@@ -252,8 +263,8 @@ def tile_swinmlpblocknew_pa_kernel(tc, x, norm1_w, norm1_b, spatial_w, spatial_b
                 )
 
         load_x(0)
-        load_x(1)
         load_weights(0, 0)
+        load_x(1)
         load_weights(0, 1)
         load_x(2)
         load_weights(1, 0)
@@ -266,6 +277,7 @@ def tile_swinmlpblocknew_pa_kernel(tc, x, norm1_w, norm1_b, spatial_w, spatial_b
         make_identity(nc, ident[:])
         nc.vector.memset(ones[:], 1.0)
         nc.vector.memset(norm_rows[:], 0.0)
+        nc.vector.tensor_scalar(out=eps_col[:], in0=ones[:, 0:1], scalar1=0.0, scalar2=EPS, op0=ALU.mult, op1=ALU.add)
         nc.gpsimd.memset(bias_rows[:], 0.0)
         nc.scalar.sqrt(out=scratch[:], in_=ones[:, 0:1])
         nc.scalar.dma_start(out=norm_rows[0:1, 0:C], in_=norm1_w.unsqueeze(0))
@@ -273,35 +285,55 @@ def tile_swinmlpblocknew_pa_kernel(tc, x, norm1_w, norm1_b, spatial_w, spatial_b
         nc.scalar.dma_start(
             out=bias_rows[0 : HEADS * PASSES, :], in_=spatial_b.rearrange("h (g k) -> (h g) k", g=PASSES)
         )
-        statistics(0)
-        deviation(0)
         transpose_items(0, range(2))
-        copy_items_out(0, range(2))
         norm_ps = psum_norm.tile([P, 2 * C], F32, tag="norm")
         nc.tensor.matmul(out=norm_ps[:], lhsT=ones[:], rhs=norm_rows[:], start=True, stop=True)
+        statistics(0, range(4))
+        copy_items_out(0, range(1))
+        deviation(0)
+        copy_items_out(0, range(1, 2))
         nc.scalar.copy(out=norm_sb[:], in_=norm_ps[:])
-        statistics(1)
-        deviation(1)
-        normalise(0)
-        gain(0, 0)
+        statistics(1, range(2))
+        inverse(0)
+        statistics(1, range(2, 3))
+        offset(0)
+        statistics(1, range(3, 4))
         transpose_items(0, range(2, ITEMS))
         load_next(0)
+        normalise(0, 0)
+        gain(0, 0)
+        deviation(1)
         copy_items_out(0, range(2, ITEMS))
+        statistics(2, range(2))
+        inverse(1)
+        statistics(2, range(2, 3))
+        offset(1)
+        statistics(2, range(3, 4))
         transpose_items(1, range(ITEMS))
         load_next(1)
-        copy_items_out(1, range(2))
-        statistics(2)
-        deviation(2)
-        normalise(1)
+        normalise(1, 0)
         gain(1, 0)
-        copy_items_out(1, range(2, ITEMS))
-        prepare_group(2)
-        statistics(3)
-        deviation(3)
-        normalise(2)
+        copy_items_out(1, range(1))
+        deviation(2)
+        copy_items_out(1, range(1, ITEMS))
+        statistics(3, range(2))
+        inverse(2)
+        statistics(3, range(2, 3))
+        offset(2)
+        statistics(3, range(3, 4))
+        normalise(2, 0)
         gain(2, 0)
-        normalise(3)
+        deviation(3)
+        shift(0, 0)
+        inverse(3)
+        shift(1, 0)
+        offset(3)
+        transpose_items(2, range(ITEMS))
+        load_next(2)
+        copy_items_out(2, range(1))
+        normalise(3, 0)
         gain(3, 0)
+        copy_items_out(2, range(1, ITEMS))
         for k in range(3, AHEAD):
             prepare_group(k)
         bias_ps = psum_words.tile([P, 2 * PASSES, P], F32, tag="words")
@@ -312,24 +344,37 @@ def tile_swinmlpblocknew_pa_kernel(tc, x, norm1_w, norm1_b, spatial_w, spatial_b
                 out=bias_col[:, PAIR * u : PAIR * (u + 1), :],
                 in_=bias_ps[:, u, 0 : HEADS * PASSES].bitcast(BF16).rearrange("p (r e) -> p e r", e=PAIR),
             )
-        shift(0, 0)
-        shift(1, 0)
         quantise_group(0)
         shift(2, 0)
+        quantise_group(1)
         shift(3, 0)
+        quantise_group(2)
         quantise_x(0)
-        for n in range(WINDOWS):
-            gain(n, 1)
 
+        layer_norm = [(n, pair) for pair in range(1, PAIRS) for n in range(WINDOWS)]
+        normalised = 0
+        shifted = 0
+        prepared = AHEAD
+        quantised = 3
         for k in range(GROUPS):
-            if k > 0:
-                quantise_group(k)
-                finish_group(k - 1)
-            if 0 < k <= WINDOWS:
-                shift(k - 1, 1)
-            if k == WINDOWS:
-                quantise_x(1)
-            if k + AHEAD < GROUPS:
-                prepare_group(k + AHEAD)
+            pair, quarter = ORDER[k]
+            due = min(len(layer_norm), WINDOWS * (k + 1) // (QUARTERS - 1))
+            if quarter == 0 and pair > 0:
+                quantise_x(pair)
+            while normalised < min(len(layer_norm), due + 1):
+                normalise(*layer_norm[normalised])
+                gain(*layer_norm[normalised])
+                normalised += 1
+            if prepared < GROUPS:
+                prepare_group(prepared)
+                prepared += 1
             multiply_group(k)
+            if k > 0:
+                finish_group(k - 1)
+            while quantised < min(GROUPS, k + 1 + LEAD):
+                quantise_group(quantised)
+                quantised += 1
+            while shifted < due:
+                shift(*layer_norm[shifted])
+                shifted += 1
         finish_group(GROUPS - 1)

@@ -23,6 +23,8 @@ PAIR = 2
 RUNS = PASSES * PACK
 PAIRS = 4
 PAIR_CH = C // PAIRS
+HALF_CH = 2 * PAIR_CH
+SCALAR_WINDOWS = (0, 1)
 HEADS_PER_PAIR = HEADS // PAIRS
 QUARTERS = 4
 ITEMS = HEADS_PER_PAIR * PAIR
@@ -73,10 +75,10 @@ def tile_swinmlpblocknew_pa_kernel(tc, x, norm1_w, norm1_b, spatial_w, spatial_b
         std = keep.tile([P, WINDOWS, RUNS], F32)
         minus_mean_rstd = keep.tile([P, WINDOWS, RUNS], F32)
         norm_sb = keep.tile([P, 2 * C], F32)
+        normed = keep.tile([P, WINDOWS, RUNS, C], F32)
         x_codes = keep.tile([P, PAIRS, PASSES, HEADS_PER_PAIR, P], U32, align_bytes=64)
         x_scales = keep.tile([P, PAIRS, PASSES, HEADS_PER_PAIR, P], U8, align_bytes=64)
 
-        normed = {}
         xn_grouped = {}
         w_raw = {}
         words_ps = {}
@@ -115,36 +117,53 @@ def tile_swinmlpblocknew_pa_kernel(tc, x, norm1_w, norm1_b, spatial_w, spatial_b
                 op1=ALU.mult,
             )
 
-        def normalise(n, pair):
-            if n == 0:
-                normed_p = norm_pool.tile([P, WINDOWS, RUNS, PAIR_CH], F32, tag="normed")
-                grouped_p = norm_pool.tile(
-                    [P, PASSES, HEADS_PER_PAIR, WINDOWS, HEAD_DIM * PACK], BF16, tag="xn_grouped", align_bytes=64
-                )
-                normed[pair] = normed_p
-                xn_grouped[pair] = grouped_p
+        def normalise_on_scalar(n, half):
+            cols = slice(half * HALF_CH, (half + 1) * HALF_CH)
             for r in range(RUNS):
                 nc.scalar.activation(
-                    out=normed[pair][:, n, r, :],
-                    in_=x_sb[:, n, r, pair * PAIR_CH : (pair + 1) * PAIR_CH],
+                    out=normed[:, n, r, cols],
+                    in_=x_sb[:, n, r, cols],
                     func=ACT.Identity,
                     scale=rstd[:, n, r : r + 1],
                     bias=minus_mean_rstd[:, n, r : r + 1],
                 )
 
-        def gain(n, pair):
-            nc.gpsimd.tensor_tensor(
-                out=normed[pair][:, n],
-                in0=normed[pair][:, n],
-                in1=norm_sb[:, pair * PAIR_CH : (pair + 1) * PAIR_CH].unsqueeze(1).to_broadcast([P, RUNS, PAIR_CH]),
+        def normalise_on_vector(n):
+            for r in range(RUNS):
+                nc.vector.tensor_scalar(
+                    out=normed[:, n, r, :],
+                    in0=x_sb[:, n, r, :],
+                    scalar1=stats[:, n, r // PAIR, 3 * (r % PAIR) + 1 : 3 * (r % PAIR) + 2],
+                    scalar2=rstd[:, n, r : r + 1],
+                    op0=ALU.subtract,
+                    op1=ALU.mult,
+                )
+
+        def gain(n, pair, engine, weights):
+            cols = slice(pair * PAIR_CH, (pair + 1) * PAIR_CH)
+            engine.tensor_tensor(
+                out=normed[:, n, :, cols],
+                in0=normed[:, n, :, cols],
+                in1=weights[:, cols].unsqueeze(1).to_broadcast([P, RUNS, PAIR_CH]),
                 op=ALU.mult,
             )
 
+        def gain_on_vector(n, pair):
+            gain(n, pair, nc.vector, norm_ps)
+
+        def gain_on_gpsimd(n, pair):
+            gain(n, pair, nc.gpsimd, norm_sb)
+
         def shift(n, pair):
+            if n == 0:
+                grouped_p = norm_pool.tile(
+                    [P, PASSES, HEADS_PER_PAIR, WINDOWS, HEAD_DIM * PACK], BF16, tag="xn_grouped", align_bytes=64
+                )
+                xn_grouped[pair] = grouped_p
             for g in range(PASSES):
                 nc.vector.tensor_tensor(
                     out=xn_grouped[pair][:, g, :, n, :].rearrange("q h (d j) -> q h d j", j=PACK),
-                    in0=normed[pair][:, n, PACK * g : PACK * (g + 1), :].rearrange("q j (h d) -> q h d j", h=HEADS_PER_PAIR),
+                    in0=normed[:, n, PACK * g : PACK * (g + 1), pair * PAIR_CH : (pair + 1) * PAIR_CH].rearrange("q j (h d) -> q h d j", h=HEADS_PER_PAIR),
                     in1=norm_ps[:, C + pair * PAIR_CH : C + (pair + 1) * PAIR_CH]
                     .rearrange("q (h d) -> q h d", h=HEADS_PER_PAIR)
                     .unsqueeze(3)
@@ -285,57 +304,54 @@ def tile_swinmlpblocknew_pa_kernel(tc, x, norm1_w, norm1_b, spatial_w, spatial_b
         nc.scalar.dma_start(
             out=bias_rows[0 : HEADS * PASSES, :], in_=spatial_b.rearrange("h (g k) -> (h g) k", g=PASSES)
         )
-        transpose_items(0, range(2))
+        transpose_items(0, range(0, 2))
         norm_ps = psum_norm.tile([P, 2 * C], F32, tag="norm")
         nc.tensor.matmul(out=norm_ps[:], lhsT=ones[:], rhs=norm_rows[:], start=True, stop=True)
-        statistics(0, range(4))
-        copy_items_out(0, range(1))
+        statistics(0, range(0, 4))
+        copy_items_out(0, range(0, 1))
         deviation(0)
         copy_items_out(0, range(1, 2))
         nc.scalar.copy(out=norm_sb[:], in_=norm_ps[:])
-        statistics(1, range(2))
+        statistics(1, range(0, 2))
         inverse(0)
         statistics(1, range(2, 3))
         offset(0)
         statistics(1, range(3, 4))
-        transpose_items(0, range(2, ITEMS))
+        transpose_items(0, range(2, 4))
         load_next(0)
-        normalise(0, 0)
-        gain(0, 0)
+        copy_items_out(0, range(2, 3))
         deviation(1)
-        copy_items_out(0, range(2, ITEMS))
-        statistics(2, range(2))
+        normalise_on_scalar(0, 0)
+        gain_on_gpsimd(0, 0)
+        statistics(2, range(0, 2))
         inverse(1)
         statistics(2, range(2, 3))
         offset(1)
         statistics(2, range(3, 4))
-        transpose_items(1, range(ITEMS))
+        transpose_items(1, range(0, 4))
         load_next(1)
-        normalise(1, 0)
-        gain(1, 0)
-        copy_items_out(1, range(1))
         deviation(2)
-        copy_items_out(1, range(1, ITEMS))
-        statistics(3, range(2))
+        copy_items_out(0, range(3, 4))
+        normalise_on_scalar(1, 0)
+        gain_on_gpsimd(1, 0)
+        statistics(3, range(0, 2))
         inverse(2)
-        statistics(3, range(2, 3))
-        offset(2)
-        statistics(3, range(3, 4))
-        normalise(2, 0)
-        gain(2, 0)
+        statistics(3, range(2, 4))
         deviation(3)
-        shift(0, 0)
-        inverse(3)
-        shift(1, 0)
-        offset(3)
-        transpose_items(2, range(ITEMS))
+        copy_items_out(1, range(0, 4))
+        transpose_items(2, range(0, 4))
         load_next(2)
-        copy_items_out(2, range(1))
-        normalise(3, 0)
-        gain(3, 0)
-        copy_items_out(2, range(1, ITEMS))
-        for k in range(3, AHEAD):
-            prepare_group(k)
+        copy_items_out(2, range(0, 4))
+        normalise_on_vector(2)
+        inverse(3)
+        normalise_on_vector(3)
+        shift(0, 0)
+        gain_on_vector(2, 0)
+        shift(1, 0)
+        gain_on_vector(3, 0)
+        shift(2, 0)
+        prepare_group(3)
+        prepare_group(4)
         bias_ps = psum_words.tile([P, 2 * PASSES, P], F32, tag="words")
         for u in range(2):
             nc.tensor.transpose(out=bias_ps[:, u, :], in_=bias_rows[:].bitcast(F32)[:, u : 2 * P : 2], identity=ident[:])
@@ -344,15 +360,14 @@ def tile_swinmlpblocknew_pa_kernel(tc, x, norm1_w, norm1_b, spatial_w, spatial_b
                 out=bias_col[:, PAIR * u : PAIR * (u + 1), :],
                 in_=bias_ps[:, u, 0 : HEADS * PASSES].bitcast(BF16).rearrange("p (r e) -> p e r", e=PAIR),
             )
-        quantise_group(0)
-        shift(2, 0)
-        quantise_group(1)
         shift(3, 0)
-        quantise_group(2)
+        quantise_group(0)
         quantise_x(0)
+        quantise_group(1)
+        quantise_group(2)
 
         layer_norm = [(n, pair) for pair in range(1, PAIRS) for n in range(WINDOWS)]
-        normalised = 0
+        gained = 0
         shifted = 0
         prepared = AHEAD
         quantised = 3
@@ -361,10 +376,11 @@ def tile_swinmlpblocknew_pa_kernel(tc, x, norm1_w, norm1_b, spatial_w, spatial_b
             due = min(len(layer_norm), WINDOWS * (k + 1) // (QUARTERS - 1))
             if quarter == 0 and pair > 0:
                 quantise_x(pair)
-            while normalised < min(len(layer_norm), due + 1):
-                normalise(*layer_norm[normalised])
-                gain(*layer_norm[normalised])
-                normalised += 1
+            if k < len(SCALAR_WINDOWS):
+                normalise_on_scalar(SCALAR_WINDOWS[k], 1)
+            while gained < min(len(layer_norm), due + 1):
+                gain_on_gpsimd(*layer_norm[gained])
+                gained += 1
             if prepared < GROUPS:
                 prepare_group(prepared)
                 prepared += 1

@@ -23,8 +23,6 @@ PAIR = 2
 RUNS = PASSES * PACK
 PAIRS = 4
 PAIR_CH = C // PAIRS
-HALF_CH = 2 * PAIR_CH
-SCALAR_WINDOWS = (0, 1)
 HEADS_PER_PAIR = HEADS // PAIRS
 QUARTERS = 4
 ITEMS = HEADS_PER_PAIR * PAIR
@@ -32,8 +30,8 @@ ORDER = [(pair, quarter) for pair in range(PAIRS) for quarter in range(QUARTERS 
     (pair, QUARTERS - 1) for pair in range(PAIRS)
 ]
 GROUPS = len(ORDER)
-AHEAD = 5
-LEAD = 4
+AHEAD = 4
+LEAD = 3
 WEIGHT_BUFS = 6
 EPS = 1e-5
 
@@ -46,7 +44,7 @@ def tile_swinmlpblocknew_pa_kernel(tc, x, norm1_w, norm1_b, spatial_w, spatial_b
         "b (wr g row wc run j) c -> (b wr) wc g row run (j c)", wr=2, g=PASSES, row=16, wc=2, run=8, j=PACK
     )
     out_by_s = out.rearrange(
-        "b (wr g row wc run i e) c -> (b wr) wc g i row run (e c)", wr=2, g=PASSES, row=16, wc=2, run=8, i=2, e=PAIR
+        "b (wr g row wc run j) c -> (b wr) wc g row run (j c)", wr=2, g=PASSES, row=16, wc=2, run=8, j=PACK
     )
     w_by_s = spatial_w.rearrange("h (g p i e) t -> h g i p (e t)", g=PASSES, p=P, i=2, e=PAIR)
 
@@ -54,9 +52,9 @@ def tile_swinmlpblocknew_pa_kernel(tc, x, norm1_w, norm1_b, spatial_w, spatial_b
         keep = ctx.enter_context(tc.tile_pool(name="keep", bufs=1))
         norm_pool = ctx.enter_context(tc.tile_pool(name="norm", bufs=2))
         weight_pool = ctx.enter_context(tc.tile_pool(name="weights", bufs=WEIGHT_BUFS))
-        grouped_pool = ctx.enter_context(tc.tile_pool(name="grouped", bufs=AHEAD))
-        codes_pool = ctx.enter_context(tc.tile_pool(name="codes", bufs=LEAD + 3))
-        out_pool = ctx.enter_context(tc.tile_pool(name="outs", bufs=QUARTERS))
+        grouped_pool = ctx.enter_context(tc.tile_pool(name="grouped", bufs=AHEAD + 1))
+        codes_pool = ctx.enter_context(tc.tile_pool(name="codes", bufs=LEAD + 4))
+        out_pool = ctx.enter_context(tc.tile_pool(name="outs", bufs=PASSES))
         psum_words = ctx.enter_context(tc.psum_pool(name="psum_words", bufs=5))
         psum_acc = ctx.enter_context(tc.psum_pool(name="psum_acc", bufs=2))
         psum_norm = ctx.enter_context(tc.psum_pool(name="psum_norm", bufs=1))
@@ -117,12 +115,11 @@ def tile_swinmlpblocknew_pa_kernel(tc, x, norm1_w, norm1_b, spatial_w, spatial_b
                 op1=ALU.mult,
             )
 
-        def normalise_on_scalar(n, half):
-            cols = slice(half * HALF_CH, (half + 1) * HALF_CH)
+        def normalise_on_scalar(n):
             for r in range(RUNS):
                 nc.scalar.activation(
-                    out=normed[:, n, r, cols],
-                    in_=x_sb[:, n, r, cols],
+                    out=normed[:, n, r, :],
+                    in_=x_sb[:, n, r, :],
                     func=ACT.Identity,
                     scale=rstd[:, n, r : r + 1],
                     bias=minus_mean_rstd[:, n, r : r + 1],
@@ -178,14 +175,15 @@ def tile_swinmlpblocknew_pa_kernel(tc, x, norm1_w, norm1_b, spatial_w, spatial_b
                 in_=xn_grouped[pair][:].rearrange("q g h n f -> q (g h n f)"),
             )
 
-        def load_weights(k, head):
+        def load_weights(k, first_head, last_head):
             heads, quarter = ORDER[k]
-            if head == 0:
-                w_raw_k = weight_pool.tile([P, 2, PAIR, TOKENS], BF16, tag="w_raw")
+            if first_head == 0:
+                w_raw_k = weight_pool.tile([P, HEADS_PER_PAIR, PAIR, TOKENS], BF16, tag="w_raw")
                 w_raw[k] = w_raw_k
             nc.sync.dma_start(
-                out=w_raw[k][:, head].rearrange("p e t -> p (e t)"),
-                in_=w_by_s[2 * heads + head, quarter // 2, quarter % 2],
+                out=w_raw[k][:, first_head:last_head].rearrange("p h e t -> p h (e t)"),
+                in_=w_by_s[HEADS_PER_PAIR * heads + first_head : HEADS_PER_PAIR * heads + last_head, quarter // 2, quarter % 2]
+                .rearrange("h p f -> p h f"),
             )
 
         def transpose_items(k, items):
@@ -213,8 +211,7 @@ def tile_swinmlpblocknew_pa_kernel(tc, x, norm1_w, norm1_b, spatial_w, spatial_b
 
         def load_next(k):
             if k + WEIGHT_BUFS < GROUPS:
-                load_weights(k + WEIGHT_BUFS, 0)
-                load_weights(k + WEIGHT_BUFS, 1)
+                load_weights(k + WEIGHT_BUFS, 0, HEADS_PER_PAIR)
 
         def prepare_group(k):
             transpose_items(k, range(ITEMS))
@@ -248,19 +245,25 @@ def tile_swinmlpblocknew_pa_kernel(tc, x, norm1_w, norm1_b, spatial_w, spatial_b
                         stop=(g == PASSES - 1),
                     )
 
+        def store(g, rows):
+            for n in range(WINDOWS):
+                nc.sync.dma_start(
+                    out=out_by_s[n // 2, n % 2, g][:, :, rows.start * C : rows.stop * C],
+                    in_=out_sb[g][:, n, rows, :].rearrange("p j c -> p (j c)"),
+                )
+
         def finish_group(k):
             heads, quarter = ORDER[k]
             g = quarter // 2
-            if heads == 0:
-                out_q = out_pool.tile([P, WINDOWS, PAIR, C], F32, tag="out_sb")
-                out_sb[quarter] = out_q
+            if g not in out_sb:
+                out_g = out_pool.tile([P, WINDOWS, PACK, C], F32, tag="out_sb")
+                out_sb[g] = out_g
             for item in range(ITEMS):
                 h = HEADS_PER_PAIR * heads + item // PAIR
-                e = item % PAIR
-                j = PAIR * (quarter % 2) + e
+                j = PAIR * (quarter % 2) + item % PAIR
                 cols = slice(h * HEAD_DIM, (h + 1) * HEAD_DIM)
                 nc.vector.scalar_tensor_tensor(
-                    out=out_sb[quarter][:, :, e, cols],
+                    out=out_sb[g][:, :, j, cols],
                     in0=acc[k][:, item, :].rearrange("p (n d) -> p n d", n=WINDOWS),
                     scalar=bias_col[:, j, PASSES * h + g : PASSES * h + g + 1],
                     in1=x_sb[:, :, PACK * g + j, cols],
@@ -268,11 +271,7 @@ def tile_swinmlpblocknew_pa_kernel(tc, x, norm1_w, norm1_b, spatial_w, spatial_b
                     op1=ALU.add,
                 )
             if heads == PAIRS - 1:
-                for n in range(WINDOWS):
-                    nc.sync.dma_start(
-                        out=out_by_s[n // 2, n % 2, quarter // 2, quarter % 2],
-                        in_=out_sb[quarter][:, n].rearrange("p e c -> p (e c)"),
-                    )
+                store(g, slice(PAIR * (quarter % 2), PAIR * (quarter % 2 + 1)))
 
         def load_x(n):
             for g in range(PASSES):
@@ -282,62 +281,57 @@ def tile_swinmlpblocknew_pa_kernel(tc, x, norm1_w, norm1_b, spatial_w, spatial_b
                 )
 
         load_x(0)
-        load_weights(0, 0)
+        nc.vector.memset(norm_rows[:], 0.0)
+        nc.vector.memset(ones[:], 1.0)
+        nc.sync.dma_start(out=norm_rows[0:1, 0:C], in_=norm1_w.unsqueeze(0))
+        nc.sync.dma_start(out=norm_rows[0:1, C : 2 * C], in_=norm1_b.unsqueeze(0))
         load_x(1)
-        load_weights(0, 1)
         load_x(2)
-        load_weights(1, 0)
+        load_weights(0, 0, 1)
         load_x(3)
-        load_weights(1, 1)
-        for k in range(2, WEIGHT_BUFS):
-            load_weights(k, 0)
-            load_weights(k, 1)
+        load_weights(0, 1, 2)
+        for k in range(1, WEIGHT_BUFS):
+            load_weights(k, 0, HEADS_PER_PAIR)
 
         make_identity(nc, ident[:])
-        nc.vector.memset(ones[:], 1.0)
-        nc.vector.memset(norm_rows[:], 0.0)
         nc.vector.tensor_scalar(out=eps_col[:], in0=ones[:, 0:1], scalar1=0.0, scalar2=EPS, op0=ALU.mult, op1=ALU.add)
         nc.gpsimd.memset(bias_rows[:], 0.0)
         nc.scalar.sqrt(out=scratch[:], in_=ones[:, 0:1])
-        nc.scalar.dma_start(out=norm_rows[0:1, 0:C], in_=norm1_w.unsqueeze(0))
-        nc.scalar.dma_start(out=norm_rows[0:1, C : 2 * C], in_=norm1_b.unsqueeze(0))
-        nc.scalar.dma_start(
+        nc.gpsimd.dma_start(
             out=bias_rows[0 : HEADS * PASSES, :], in_=spatial_b.rearrange("h (g k) -> (h g) k", g=PASSES)
         )
-        transpose_items(0, range(0, 2))
         norm_ps = psum_norm.tile([P, 2 * C], F32, tag="norm")
         nc.tensor.matmul(out=norm_ps[:], lhsT=ones[:], rhs=norm_rows[:], start=True, stop=True)
-        statistics(0, range(0, 4))
-        copy_items_out(0, range(0, 1))
-        deviation(0)
-        copy_items_out(0, range(1, 2))
         nc.scalar.copy(out=norm_sb[:], in_=norm_ps[:])
+        statistics(0, range(0, 4))
+        deviation(0)
         statistics(1, range(0, 2))
         inverse(0)
         statistics(1, range(2, 3))
         offset(0)
         statistics(1, range(3, 4))
-        transpose_items(0, range(2, 4))
-        load_next(0)
-        copy_items_out(0, range(2, 3))
         deviation(1)
-        normalise_on_scalar(0, 0)
+        normalise_on_scalar(0)
         gain_on_gpsimd(0, 0)
         statistics(2, range(0, 2))
         inverse(1)
         statistics(2, range(2, 3))
         offset(1)
         statistics(2, range(3, 4))
-        transpose_items(1, range(0, 4))
-        load_next(1)
         deviation(2)
-        copy_items_out(0, range(3, 4))
-        normalise_on_scalar(1, 0)
+        normalise_on_scalar(1)
         gain_on_gpsimd(1, 0)
         statistics(3, range(0, 2))
         inverse(2)
         statistics(3, range(2, 4))
         deviation(3)
+        transpose_items(0, range(0, 2))
+        copy_items_out(0, range(0, 2))
+        transpose_items(0, range(2, 4))
+        load_next(0)
+        copy_items_out(0, range(2, 4))
+        transpose_items(1, range(0, 4))
+        load_next(1)
         copy_items_out(1, range(0, 4))
         transpose_items(2, range(0, 4))
         load_next(2)
@@ -351,7 +345,6 @@ def tile_swinmlpblocknew_pa_kernel(tc, x, norm1_w, norm1_b, spatial_w, spatial_b
         gain_on_vector(3, 0)
         shift(2, 0)
         prepare_group(3)
-        prepare_group(4)
         bias_ps = psum_words.tile([P, 2 * PASSES, P], F32, tag="words")
         for u in range(2):
             nc.tensor.transpose(out=bias_ps[:, u, :], in_=bias_rows[:].bitcast(F32)[:, u : 2 * P : 2], identity=ident[:])
@@ -376,8 +369,6 @@ def tile_swinmlpblocknew_pa_kernel(tc, x, norm1_w, norm1_b, spatial_w, spatial_b
             due = min(len(layer_norm), WINDOWS * (k + 1) // (QUARTERS - 1))
             if quarter == 0 and pair > 0:
                 quantise_x(pair)
-            if k < len(SCALAR_WINDOWS):
-                normalise_on_scalar(SCALAR_WINDOWS[k], 1)
             while gained < min(len(layer_norm), due + 1):
                 gain_on_gpsimd(*layer_norm[gained])
                 gained += 1

@@ -157,16 +157,18 @@ def tile_swinmlpblocknew_pa_kernel(tc, x, norm1_w, norm1_b, spatial_w, spatial_b
                     [P, PASSES, HEADS_PER_PAIR, WINDOWS, HEAD_DIM * PACK], BF16, tag="xn_grouped", align_bytes=64
                 )
                 xn_grouped[pair] = grouped_p
-            for g in range(PASSES):
-                nc.vector.tensor_tensor(
-                    out=xn_grouped[pair][:, g, :, n, :].rearrange("q h (d j) -> q h d j", j=PACK),
-                    in0=normed[:, n, PACK * g : PACK * (g + 1), pair * PAIR_CH : (pair + 1) * PAIR_CH].rearrange("q j (h d) -> q h d j", h=HEADS_PER_PAIR),
-                    in1=norm_ps[:, C + pair * PAIR_CH : C + (pair + 1) * PAIR_CH]
-                    .rearrange("q (h d) -> q h d", h=HEADS_PER_PAIR)
-                    .unsqueeze(3)
-                    .to_broadcast([P, HEADS_PER_PAIR, HEAD_DIM, PACK]),
-                    op=ALU.add,
-                )
+            nc.vector.tensor_tensor(
+                out=xn_grouped[pair][:, :, :, n, :].rearrange("q g h (d j) -> q g h d j", j=PACK),
+                in0=normed[:, n, :, pair * PAIR_CH : (pair + 1) * PAIR_CH].rearrange(
+                    "q (g j) (h d) -> q g h d j", g=PASSES, h=HEADS_PER_PAIR
+                ),
+                in1=norm_ps[:, C + pair * PAIR_CH : C + (pair + 1) * PAIR_CH]
+                .rearrange("q (h d) -> q h d", h=HEADS_PER_PAIR)
+                .unsqueeze(1)
+                .unsqueeze(4)
+                .to_broadcast([P, PASSES, HEADS_PER_PAIR, HEAD_DIM, PACK]),
+                op=ALU.add,
+            )
 
         def quantise_x(pair):
             nc.vector.quantize_mx(
@@ -287,8 +289,8 @@ def tile_swinmlpblocknew_pa_kernel(tc, x, norm1_w, norm1_b, spatial_w, spatial_b
         nc.sync.dma_start(out=norm_rows[0:1, C : 2 * C], in_=norm1_b.unsqueeze(0))
         load_x(1)
         load_x(2)
-        load_weights(0, 0, 1)
         load_x(3)
+        load_weights(0, 0, 1)
         load_weights(0, 1, 2)
         for k in range(1, WEIGHT_BUFS):
             load_weights(k, 0, HEADS_PER_PAIR)

from contextlib import ExitStack

import concourse.mybir as mybir
from concourse.masks import make_identity

F32 = mybir.dt.float32
BF16 = mybir.dt.bfloat16
U32 = mybir.dt.uint32
U8 = mybir.dt.uint8
FP8X4 = mybir.dt.float8_e4m3fn_x4
ALU = mybir.AluOpType
ACT = mybir.ActivationFunctionType

P = 128
C = 256
HEADS = 8
HEAD_DIM = C // HEADS
WINDOWS = 4
TOKENS = 1024
PASSES = 2
PACK = 4
PAIR = 2
RUNS = PASSES * PACK
PAIRS = 4
PAIR_CH = C // PAIRS
HEADS_PER_PAIR = HEADS // PAIRS
QUARTERS = 4
ITEMS = HEADS_PER_PAIR * PAIR
ORDER = [(pair, quarter) for pair in range(PAIRS) for quarter in range(QUARTERS - 1)] + [
    (pair, QUARTERS - 1) for pair in range(PAIRS)
]
GROUPS = len(ORDER)
AHEAD = 4
LEAD = 3
WEIGHT_BUFS = 6
EPS = 1e-5

FLOPS = 2 * HEADS * WINDOWS * TOKENS * TOKENS * HEAD_DIM


def tile_swinmlpblocknew_pa_kernel(tc, x, norm1_w, norm1_b, spatial_w, spatial_b, out):
    nc = tc.nc
    x_by_t = x.rearrange(
        "b (wr g row wc run j) c -> (b wr) wc g row run (j c)", wr=2, g=PASSES, row=16, wc=2, run=8, j=PACK
    )
    out_by_s = out.rearrange(
        "b (wr g row wc run j) c -> (b wr) wc g row run (j c)", wr=2, g=PASSES, row=16, wc=2, run=8, j=PACK
    )
    w_by_s = spatial_w.rearrange("h (g p i e) t -> h g i p (e t)", g=PASSES, p=P, i=2, e=PAIR)

    with ExitStack() as ctx:
        keep = ctx.enter_context(tc.tile_pool(name="keep", bufs=1))
        norm_pool = ctx.enter_context(tc.tile_pool(name="norm", bufs=2))
        weight_pool = ctx.enter_context(tc.tile_pool(name="weights", bufs=WEIGHT_BUFS))
        grouped_pool = ctx.enter_context(tc.tile_pool(name="grouped", bufs=AHEAD + 1))
        codes_pool = ctx.enter_context(tc.tile_pool(name="codes", bufs=LEAD + 4))
        out_pool = ctx.enter_context(tc.tile_pool(name="outs", bufs=PASSES))
        psum_words = ctx.enter_context(tc.psum_pool(name="psum_words", bufs=5))
        psum_acc = ctx.enter_context(tc.psum_pool(name="psum_acc", bufs=2))
        psum_norm = ctx.enter_context(tc.psum_pool(name="psum_norm", bufs=1))
        ctx.enter_context(tc.manual_schedule())

        x_sb = keep.tile([P, WINDOWS, RUNS, C], BF16)
        ident = keep.tile([P, P], F32)
        ones = keep.tile([P, P], BF16)
        norm_rows = keep.tile([P, 2 * C], BF16)
        scratch = keep.tile([P, 1], F32)
        bias_rows = keep.tile([P, PASSES * P * PACK // PASSES], BF16)
        bias_col = keep.tile([P, PACK, HEADS * PASSES], F32)
        stats = keep.tile([P, WINDOWS, RUNS // PAIR, 3 * PAIR], F32)
        eps_col = keep.tile([P, 1], F32)
        rstd = keep.tile([P, WINDOWS, RUNS], F32)
        std = keep.tile([P, WINDOWS, RUNS], F32)
        minus_mean_rstd = keep.tile([P, WINDOWS, RUNS], F32)
        norm_sb = keep.tile([P, 2 * C], F32)
        normed = keep.tile([P, WINDOWS, RUNS, C], F32)
        x_codes = keep.tile([P, PAIRS, PASSES, HEADS_PER_PAIR, P], U32, align_bytes=64)
        x_scales = keep.tile([P, PAIRS, PASSES, HEADS_PER_PAIR, P], U8, align_bytes=64)

        xn_grouped = {}
        w_raw = {}
        words_ps = {}
        w_grouped = {}
        w_codes = {}
        w_scales = {}
        acc = {}
        out_sb = {}

        def moments(n, k):
            return stats[:, n, :, :].rearrange("q a (e k) -> q a e k", k=3)[:, :, :, k]

        def pairs(values, n):
            return values[:, n, :].rearrange("q (a e) -> q a e", e=PAIR)

        def statistics(n, pairs_of_tokens):
            for a in pairs_of_tokens:
                nc.vector.bn_stats(
                    out=stats[:, n, a, :],
                    in_=x_sb[:, n, PAIR * a : PAIR * (a + 1), :].rearrange("q e c -> q c e"),
                )

        def deviation(n):
            nc.scalar.activation(out=pairs(std, n), in_=moments(n, 2), func=ACT.Sqrt, scale=1.0 / C, bias=eps_col[:])

        def inverse(n):
            nc.vector.reciprocal(out=rstd[:, n, :], in_=std[:, n, :])

        def offset(n):
            nc.vector.scalar_tensor_tensor(
                out=pairs(minus_mean_rstd, n),
                in0=moments(n, 1),
                scalar=-1.0,
                in1=pairs(rstd, n),
                op0=ALU.mult,
                op1=ALU.mult,
            )

        def normalise_on_scalar(n):
            for r in range(RUNS):
                nc.scalar.activation(
                    out=normed[:, n, r, :],
                    in_=x_sb[:, n, r, :],
                    func=ACT.Identity,
                    scale=rstd[:, n, r : r + 1],
                    bias=minus_mean_rstd[:, n, r : r + 1],
                )

        def normalise_on_vector(n):
            for r in range(RUNS):
                nc.vector.tensor_scalar(
                    out=normed[:, n, r, :],
                    in0=x_sb[:, n, r, :],
                    scalar1=stats[:, n, r // PAIR, 3 * (r % PAIR) + 1 : 3 * (r % PAIR) + 2],
                    scalar2=rstd[:, n, r : r + 1],
                    op0=ALU.subtract,
                    op1=ALU.mult,
                )

        def gain(n, pair, engine, weights):
            cols = slice(pair * PAIR_CH, (pair + 1) * PAIR_CH)
            engine.tensor_tensor(
                out=normed[:, n, :, cols],
                in0=normed[:, n, :, cols],
                in1=weights[:, cols].unsqueeze(1).to_broadcast([P, RUNS, PAIR_CH]),
                op=ALU.mult,
            )

        def gain_on_vector(n, pair):
            gain(n, pair, nc.vector, norm_ps)

        def gain_on_gpsimd(n, pair):
            gain(n, pair, nc.gpsimd, norm_sb)

        def shift(n, pair):
            if n == 0:
                grouped_p = norm_pool.tile(
                    [P, PASSES, HEADS_PER_PAIR, WINDOWS, HEAD_DIM * PACK], BF16, tag="xn_grouped", align_bytes=64
                )
                xn_grouped[pair] = grouped_p
            nc.vector.tensor_tensor(
                out=xn_grouped[pair][:, :, :, n, :].rearrange("q g h (d j) -> q g h d j", j=PACK),
                in0=normed[:, n, :, pair * PAIR_CH : (pair + 1) * PAIR_CH].rearrange(
                    "q (g j) (h d) -> q g h d j", g=PASSES, h=HEADS_PER_PAIR
                ),
                in1=norm_ps[:, C + pair * PAIR_CH : C + (pair + 1) * PAIR_CH]
                .rearrange("q (h d) -> q h d", h=HEADS_PER_PAIR)
                .unsqueeze(1)
                .unsqueeze(4)
                .to_broadcast([P, PASSES, HEADS_PER_PAIR, HEAD_DIM, PACK]),
                op=ALU.add,
            )

        def quantise_x(pair):
            nc.vector.quantize_mx(
                out=x_codes[:, pair].rearrange("q g h f -> q (g h f)").bitcast(FP8X4),
                scales=x_scales[:, pair].rearrange("q g h f -> q (g h f)"),
                in_=xn_grouped[pair][:].rearrange("q g h n f -> q (g h n f)"),
            )

        def load_weights(k, first_head, last_head):
            heads, quarter = ORDER[k]
            if first_head == 0:
                w_raw_k = weight_pool.tile([P, HEADS_PER_PAIR, PAIR, TOKENS], BF16, tag="w_raw")
                w_raw[k] = w_raw_k
            nc.sync.dma_start(
                out=w_raw[k][:, first_head:last_head].rearrange("p h e t -> p h (e t)"),
                in_=w_by_s[HEADS_PER_PAIR * heads + first_head : HEADS_PER_PAIR * heads + last_head, quarter // 2, quarter % 2]
                .rearrange("h p f -> p h f"),
            )

        def transpose_items(k, items):
            for item in items:
                row_words = w_raw[k][:, item // PAIR, item % PAIR, :].bitcast(F32)
                bank = psum_words.tile([P, 2 * PASSES, P], F32, tag="words")
                words_ps[k, item] = bank
                for g in range(PASSES):
                    for u in range(2):
                        nc.tensor.transpose(
                            out=bank[:, 2 * g + u, :],
                            in_=row_words[:, 2 * P * g + u : 2 * P * (g + 1) : 2],
                            identity=ident[:],
                        )

        def copy_items_out(k, items):
            if k not in w_grouped:
                grouped_k = grouped_pool.tile([P, ITEMS, PASSES * P * PACK], BF16, tag="w_grouped", align_bytes=64)
                w_grouped[k] = grouped_k
            for item in items:
                nc.scalar.copy(
                    out=w_grouped[k][:, item, :].bitcast(F32).rearrange("q (g s u) -> q g s u", g=PASSES, u=2),
                    in_=words_ps[k, item][:].rearrange("q (g u) s -> q g s u", g=PASSES),
                )

        def load_next(k):
            if k + WEIGHT_BUFS < GROUPS:
                load_weights(k + WEIGHT_BUFS, 0, HEADS_PER_PAIR)

        def prepare_group(k):
            transpose_items(k, range(ITEMS))
            load_next(k)
            copy_items_out(k, range(ITEMS))

        def quantise_group(k):
            codes_k = codes_pool.tile([P, ITEMS, PASSES, P], U32, tag="w_codes", align_bytes=64)
            scales_k = codes_pool.tile([P, ITEMS, PASSES, P], U8, tag="w_scales", align_bytes=64)
            w_codes[k] = codes_k
            w_scales[k] = scales_k
            nc.vector.quantize_mx(
                out=codes_k[:].rearrange("q i g s -> q (i g s)").bitcast(FP8X4),
                scales=scales_k[:].rearrange("q i g s -> q (i g s)"),
                in_=w_grouped[k][:].rearrange("q i f -> q (i f)"),
            )

        def multiply_group(k):
            heads, quarter = ORDER[k]
            acc_k = psum_acc.tile([P, ITEMS, P], F32, tag="acc")
            acc[k] = acc_k
            for item in range(ITEMS):
                for g in range(PASSES):
                    nc.tensor.matmul_mx(
                        out=acc_k[:, item, :],
                        lhsT=w_codes[k][:, item, g, :].bitcast(FP8X4),
                        lhsT_scale=w_scales[k][:, item, g, :],
                        rhs=x_codes[:, heads, g, item // PAIR, :].bitcast(FP8X4),
                        rhs_scale=x_scales[:, heads, g, item // PAIR, :],
                        start=(g == 0),
                        stop=(g == PASSES - 1),
                    )

        def store(g, rows):
            for n in range(WINDOWS):
                nc.sync.dma_start(
                    out=out_by_s[n // 2, n % 2, g][:, :, rows.start * C : rows.stop * C],
                    in_=out_sb[g][:, n, rows, :].rearrange("p j c -> p (j c)"),
                )

        def finish_group(k):
            heads, quarter = ORDER[k]
            g = quarter // 2
            if g not in out_sb:
                out_g = out_pool.tile([P, WINDOWS, PACK, C], F32, tag="out_sb")
                out_sb[g] = out_g
            for item in range(ITEMS):
                h = HEADS_PER_PAIR * heads + item // PAIR
                j = PAIR * (quarter % 2) + item % PAIR
                cols = slice(h * HEAD_DIM, (h + 1) * HEAD_DIM)
                nc.vector.scalar_tensor_tensor(
                    out=out_sb[g][:, :, j, cols],
                    in0=acc[k][:, item, :].rearrange("p (n d) -> p n d", n=WINDOWS),
                    scalar=bias_col[:, j, PASSES * h + g : PASSES * h + g + 1],
                    in1=x_sb[:, :, PACK * g + j, cols],
                    op0=ALU.add,
                    op1=ALU.add,
                )
            if heads == PAIRS - 1:
                store(g, slice(PAIR * (quarter % 2), PAIR * (quarter % 2 + 1)))

        def load_x(n):
            for g in range(PASSES):
                nc.sync.dma_start(
                    out=x_sb[:, n, PACK * g : PACK * (g + 1), :].rearrange("q j c -> q (j c)"),
                    in_=x_by_t[n // 2, n % 2, g],
                )

        load_x(0)
        nc.vector.memset(norm_rows[:], 0.0)
        nc.vector.memset(ones[:], 1.0)
        nc.sync.dma_start(out=norm_rows[0:1, 0:C], in_=norm1_w.unsqueeze(0))
        nc.sync.dma_start(out=norm_rows[0:1, C : 2 * C], in_=norm1_b.unsqueeze(0))
        load_x(1)
        load_x(2)
        load_x(3)
        load_weights(0, 0, 1)
        load_weights(0, 1, 2)
        for k in range(1, WEIGHT_BUFS):
            load_weights(k, 0, HEADS_PER_PAIR)

        make_identity(nc, ident[:])
        nc.vector.tensor_scalar(out=eps_col[:], in0=ones[:, 0:1], scalar1=0.0, scalar2=EPS, op0=ALU.mult, op1=ALU.add)
        nc.gpsimd.memset(bias_rows[:], 0.0)
        nc.scalar.sqrt(out=scratch[:], in_=ones[:, 0:1])
        nc.gpsimd.dma_start(
            out=bias_rows[0 : HEADS * PASSES, :], in_=spatial_b.rearrange("h (g k) -> (h g) k", g=PASSES)
        )
        norm_ps = psum_norm.tile([P, 2 * C], F32, tag="norm")
        nc.tensor.matmul(out=norm_ps[:], lhsT=ones[:], rhs=norm_rows[:], start=True, stop=True)
        nc.scalar.copy(out=norm_sb[:], in_=norm_ps[:])
        statistics(0, range(0, 4))
        deviation(0)
        statistics(1, range(0, 2))
        inverse(0)
        statistics(1, range(2, 3))
        offset(0)
        statistics(1, range(3, 4))
        deviation(1)
        normalise_on_scalar(0)
        gain_on_gpsimd(0, 0)
        statistics(2, range(0, 2))
        inverse(1)
        statistics(2, range(2, 3))
        offset(1)
        statistics(2, range(3, 4))
        deviation(2)
        normalise_on_scalar(1)
        gain_on_gpsimd(1, 0)
        statistics(3, range(0, 2))
        inverse(2)
        statistics(3, range(2, 4))
        deviation(3)
        transpose_items(0, range(0, 2))
        copy_items_out(0, range(0, 2))
        transpose_items(0, range(2, 4))
        load_next(0)
        copy_items_out(0, range(2, 4))
        transpose_items(1, range(0, 4))
        load_next(1)
        copy_items_out(1, range(0, 4))
        transpose_items(2, range(0, 4))
        load_next(2)
        copy_items_out(2, range(0, 4))
        normalise_on_vector(2)
        inverse(3)
        normalise_on_vector(3)
        shift(0, 0)
        gain_on_vector(2, 0)
        shift(1, 0)
        gain_on_vector(3, 0)
        shift(2, 0)
        prepare_group(3)
        bias_ps = psum_words.tile([P, 2 * PASSES, P], F32, tag="words")
        for u in range(2):
            nc.tensor.transpose(out=bias_ps[:, u, :], in_=bias_rows[:].bitcast(F32)[:, u : 2 * P : 2], identity=ident[:])
        for u in range(2):
            nc.scalar.copy(
                out=bias_col[:, PAIR * u : PAIR * (u + 1), :],
                in_=bias_ps[:, u, 0 : HEADS * PASSES].bitcast(BF16).rearrange("p (r e) -> p e r", e=PAIR),
            )
        shift(3, 0)
        quantise_group(0)
        quantise_x(0)
        quantise_group(1)
        quantise_group(2)

        layer_norm = [(n, pair) for pair in range(1, PAIRS) for n in range(WINDOWS)]
        gained = 0
        shifted = 0
        prepared = AHEAD
        quantised = 3
        for k in range(GROUPS):
            pair, quarter = ORDER[k]
            due = min(len(layer_norm), WINDOWS * (k + 1) // (QUARTERS - 1))
            if quarter == 0 and pair > 0:
                quantise_x(pair)
            while gained < min(len(layer_norm), due + 1):
                gain_on_gpsimd(*layer_norm[gained])
                gained += 1
            if prepared < GROUPS:
                prepare_group(prepared)
                prepared += 1
            multiply_group(k)
            if k > 0:
                finish_group(k - 1)
            while quantised < min(GROUPS, k + 1 + LEAD):
                quantise_group(quantised)
                quantised += 1
            while shifted < due:
                shift(*layer_norm[shifted])
                shifted += 1
        finish_group(GROUPS - 1)
